import numpy as np
import ml_dtypes


def mxq(x, axis, fmt="e4m3"):
    dtype, down = {"e4m3": (ml_dtypes.float8_e4m3fn, 7), "e5m2": (ml_dtypes.float8_e5m2, 14)}[fmt]
    v = np.moveaxis(np.asarray(x, np.float32).astype(ml_dtypes.bfloat16).astype(np.float64), axis, -1)
    blocks = v.reshape(v.shape[:-1] + (-1, 32))
    amax = np.abs(blocks).max(-1, keepdims=True)
    byte = np.maximum(np.where(amax > 0, np.frexp(amax)[1] - 1 + 127, 0) - down, 1)
    scale = np.exp2(byte - 127.0)
    codes = (blocks / scale).astype(np.float32).astype(dtype).astype(np.float64)
    return np.moveaxis((codes * scale).reshape(v.shape), -1, axis)


WIDE = False


def mx_kscale(k):
    if not WIDE:
        return np.ones(k)
    levels = np.array([10, -10, 5, -5, 0])
    a = np.random.permutation(np.resize(levels, k // 512 * 4)).reshape(k // 512, 4)
    idx = np.arange(k)
    return np.exp2(a[idx // 512, idx % 128 // 32])


BF16 = ml_dtypes.bfloat16


def bf(x):
    return np.asarray(x, np.float32).astype(BF16)


def f64(x):
    return np.asarray(x).astype(np.float64)


E2M1 = np.array([0.0, 0.5, 1.0, 1.5, 2.0, 3.0, 4.0, 6.0, -0.0, -0.5, -1.0, -1.5, -2.0, -3.0, -4.0, -6.0])


def pack_weight(w, fmt):
    k, n = w.shape
    w = f64(bf(w)).reshape(k // 32, 32, n)
    amax = np.abs(w).max(1)
    if fmt == "e4m3":
        byte = np.frexp(amax)[1] - 1 + 127 - 7
    else:
        mant, ex = np.frexp(amax / 6.0)
        byte = np.where(mant > 0.5, ex, ex - 1) + 127
    byte = np.clip(np.where(amax > 0, byte, 1), 1, 254)
    scaled = (w * np.exp2(127.0 - byte)[:, None, :]).reshape(k, n).astype(np.float32)
    by_word = np.ascontiguousarray(scaled.reshape(k // 512, 128, 4, n).transpose(0, 1, 3, 2))
    if fmt == "e4m3":
        words = by_word.astype(ml_dtypes.float8_e4m3fn).view(np.uint8)
    else:
        c = by_word.astype(ml_dtypes.float4_e2m1fn).view(np.uint8) & 0xF
        words = c[..., 0::2] | (c[..., 1::2] << 4)
    return np.ascontiguousarray(words), np.ascontiguousarray(byte.astype(np.uint8).reshape(k // 512, 16, n))


def unpack_weight(words, scales, fmt):
    g, p, n, _ = words.shape
    if fmt == "e4m3":
        vals = np.ascontiguousarray(words).view(ml_dtypes.float8_e4m3fn).astype(np.float64)
    else:
        nib = np.empty((g, p, n, 4), np.uint8)
        nib[..., 0::2] = words & 0xF
        nib[..., 1::2] = words >> 4
        vals = E2M1[nib]
    vals = vals * np.repeat(np.exp2(scales.astype(np.float64) - 127.0), 8, axis=1)[..., None]
    return vals.transpose(0, 1, 3, 2).reshape(g * 512, n)


B, N, P, C, HID, NB, E, MAXLEN = 2, 64, 3, 256, 128, 63, 512, 2056
EPS = 1e-5
FMT = "e4m3"


def setup_inputs():
    s, t = mx_kscale(E), mx_kscale(E)
    h1 = bf(np.maximum(np.random.standard_normal((B, N, N, E)), 0.0) * s)
    edge_mask = bf(np.random.random((B, N, N)) > 0.15)
    W2_words, W2_scales = pack_weight(np.random.standard_normal((E, E)) * 1.4 / np.sqrt(E) / s[:, None] * t, FMT)
    b2 = bf(np.random.standard_normal(E) * 0.3 * t)
    W3_words, W3_scales = pack_weight(np.random.standard_normal((E, E)) * 1.4 / np.sqrt(E) / t[:, None], FMT)
    b3 = bf(np.random.standard_normal(E) * 0.3)
    ln_g = bf(1.0 + 0.2 * np.random.standard_normal(E))
    ln_b = bf(0.2 * np.random.standard_normal(E))
    return {"h1": h1,
            "edge_mask": edge_mask,
            "W2_words": W2_words,
            "W2_scales": W2_scales,
            "b2": b2,
            "W3_words": W3_words,
            "W3_scales": W3_scales,
            "b3": b3,
            "ln_g": ln_g,
            "ln_b": ln_b}


def reference(h1, edge_mask, W2_words, W2_scales, b2, W3_words, W3_scales, b3, ln_g, ln_b):
    h = np.maximum((mxq(f64(h1), 3, "e4m3") @ unpack_weight(W2_words, W2_scales, FMT)) + f64(b2), 0.0)
    h = (mxq(h, 3, "e4m3") @ unpack_weight(W3_words, W3_scales, FMT)) + f64(b3)
    mu = h.mean(-1, keepdims=True)
    var = h.var(-1, keepdims=True)
    h = (h - mu) / np.sqrt(var + EPS) * f64(ln_g) + f64(ln_b)
    return h * f64(edge_mask)[..., None]

@@ -1,0 +1,221 @@
+import concourse.mybir as mybir
+from concourse.masks import make_identity
+
+F32 = mybir.dt.float32
+BF16 = mybir.dt.bfloat16
+I32 = mybir.dt.int32
+U32 = mybir.dt.uint32
+U8 = mybir.dt.uint8
+FP8X4 = mybir.dt.float8_e4m3fn_x4
+ALU = mybir.AluOpType
+ACT = mybir.ActivationFunctionType
+
+P = 128
+PACK = 4
+E = 512
+TOKENS = 2 * 64 * 64
+TILES = TOKENS // P
+PAIR = 2
+TILES_PER_LOAD = 8
+EPS = 1e-5
+
+FLOPS = 2 * 2 * TOKENS * E * E
+
+
+def load_weight(nc, keep, words_dram, scales_dram, name):
+    words = keep.tile([P, PACK * E], U8, name=name + "_words", align_bytes=64)
+    nc.sync.dma_start(
+        out=words[:].bitcast(I32),
+        in_=words_dram.rearrange("g p n t -> (g p) (n t)").bitcast(I32),
+    )
+    plane = keep.tile([P, E], U8, name=name + "_plane", align_bytes=64)
+    nc.vector.memset(plane[:].bitcast(I32), 0)
+    for quadrant in range(4):
+        nc.sync.dma_start(
+            out=plane[32 * quadrant : 32 * quadrant + 4, :].bitcast(I32),
+            in_=scales_dram[0, 4 * quadrant : 4 * quadrant + 4, :].bitcast(I32),
+        )
+    return words, plane
+
+
+def load_row_to_all_partitions(nc, keep, vector_dram, name):
+    row = keep.tile([P, E], BF16, name=name)
+    nc.scalar.dma_start(out=row[:], in_=vector_dram.partition_broadcast(P))
+    return row
+
+
+def quantise_pair(nc, pool, grouped, name):
+    codes = pool.tile([P, PAIR * P], U32, name=name + "_codes", align_bytes=64)
+    scales = pool.tile([P, PAIR * P], U8, name=name + "_scales", align_bytes=64)
+    nc.vector.quantize_mx(out=codes[:].bitcast(FP8X4), scales=scales[:], in_=grouped[:])
+    return codes, scales
+
+
+def tile_edgefeaturenet_pb_t_kernel(
+    tc, h1, edge_mask, W2_words, W2_scales, b2, W3_words, W3_scales, b3, ln_g, ln_b, out
+):
+    nc = tc.nc
+    h1_rows = h1.flatten_outer_dims().rearrange("(p i) k -> p i k", i=TILES)
+    out_rows = out.flatten_outer_dims().rearrange("(p i) n -> p i n", i=TILES)
+    mask_rows = edge_mask.rearrange("b r c -> (b r c)").rearrange("(p i) -> p i", i=TILES)
+
+    with tc.tile_pool(name="keep", bufs=1) as keep, tc.tile_pool(
+        name="loads", bufs=3
+    ) as loads, tc.tile_pool(name="work", bufs=3) as work, tc.tile_pool(
+        name="stats", bufs=4
+    ) as stats, tc.psum_pool(name="psum_t", bufs=1) as psum_t, tc.psum_pool(
+        name="psum_x", bufs=3
+    ) as psum_x, tc.psum_pool(name="psum_y", bufs=3) as psum_y:
+        eps = keep.tile([P, 1], F32, name="eps")
+        nc.vector.memset(eps[:], EPS)
+        warm = keep.tile([P, 1], F32, name="warm")
+        nc.scalar.activation(out=warm[:], in_=eps[:], func=ACT.Sqrt)
+
+        w2_words, w2_plane = load_weight(nc, keep, W2_words, W2_scales, "w2")
+        b2_row = load_row_to_all_partitions(nc, keep, b2, "b2_row")
+        w3_words, w3_plane = load_weight(nc, keep, W3_words, W3_scales, "w3")
+        b3_row = load_row_to_all_partitions(nc, keep, b3, "b3_row")
+        g_row = load_row_to_all_partitions(nc, keep, ln_g, "g_row")
+        beta_row = load_row_to_all_partitions(nc, keep, ln_b, "beta_row")
+
+        mask_bf = keep.tile([P, TILES], BF16, name="mask_bf")
+        nc.scalar.dma_start(out=mask_bf[:], in_=mask_rows)
+        mask = keep.tile([P, TILES], F32, name="mask")
+        nc.vector.tensor_copy(out=mask[:], in_=mask_bf[:])
+
+        ident_f32 = keep.tile([P, P], F32, name="ident_f32")
+        make_identity(nc, ident_f32[:])
+        ident_bf = keep.tile([P, P], BF16, name="ident_bf")
+        make_identity(nc, ident_bf[:])
+
+        b2_sorted = keep.tile([P, PACK, P], BF16, name="b2_sorted")
+        nc.vector.tensor_copy(
+            out=b2_sorted[:], in_=b2_row[:].rearrange("p (m t) -> p t m", t=PACK)
+        )
+
+        for first in range(0, TILES, PAIR):
+            if first % TILES_PER_LOAD == 0:
+                h1_sb = loads.tile([P, TILES_PER_LOAD, E], BF16, name="h1_sb")
+                nc.sync.dma_start(
+                    out=h1_sb[:], in_=h1_rows[:, first : first + TILES_PER_LOAD, :]
+                )
+
+            h1T = psum_t.tile([P, PAIR, 2, P], F32, name="h1T")
+            for r in range(PAIR):
+                words = h1_sb[:, first % TILES_PER_LOAD + r, :].bitcast(F32)
+                for u in range(2):
+                    nc.tensor.transpose(h1T[:, r, u, :], words[:, u : E // 2 : 2], ident_f32[:])
+            h1_grouped = work.tile([P, PAIR * P * PACK], BF16, name="h1_grouped", align_bytes=64)
+            nc.scalar.copy(
+                out=h1_grouped[:].bitcast(F32).rearrange("p (r w u) -> p r w u", r=PAIR, u=2),
+                in_=h1T[:].rearrange("p r u w -> p r w u"),
+            )
+            h1_codes, h1_scales = quantise_pair(nc, work, h1_grouped, "h1")
+
+            h_sorted = work.tile([P, PAIR, PACK, P], BF16, name="h_sorted")
+            for r in range(PAIR):
+                token_cols = slice(r * P, (r + 1) * P)
+                x1 = psum_x.tile([P, E], F32, name="x1")
+                nc.tensor.matmul_mx(
+                    out=x1[:],
+                    lhsT=h1_codes[:, token_cols].bitcast(FP8X4),
+                    lhsT_scale=h1_scales[:, token_cols],
+                    rhs=w2_words[:].bitcast(FP8X4),
+                    rhs_scale=w2_plane[:],
+                    start=True,
+                    stop=True,
+                )
+                nc.vector.tensor_tensor(
+                    out=h_sorted[:, r, :, :],
+                    in0=x1[:].rearrange("p (m t) -> p t m", t=PACK),
+                    in1=b2_sorted[:],
+                    op=ALU.add,
+                )
+
+            hT = psum_t.tile([P, PAIR, PACK, P], BF16, name="hT")
+            for r in range(PAIR):
+                for t in range(PACK):
+                    nc.tensor.transpose(hT[:, r, t, :], h_sorted[:, r, t, :], ident_bf[:])
+            h_grouped = work.tile([P, PAIR * P * PACK], BF16, name="h_grouped", align_bytes=64)
+            nc.scalar.activation(
+                out=h_grouped[:].rearrange("p (r w t) -> p r w t", r=PAIR, t=PACK),
+                in_=hT[:].rearrange("p r t w -> p r w t"),
+                func=ACT.Relu,
+            )
+            h_codes, h_scales = quantise_pair(nc, work, h_grouped, "h")
+
+            y = work.tile([P, PAIR, E], F32, name="y")
+            y_sum = stats.tile([P, PAIR], F32, name="y_sum")
+            for r in range(PAIR):
+                token_cols = slice(r * P, (r + 1) * P)
+                x2 = psum_y.tile([P, E], F32, name="x2")
+                nc.tensor.matmul_mx(
+                    out=x2[:],
+                    lhsT=h_codes[:, token_cols].bitcast(FP8X4),
+                    lhsT_scale=h_scales[:, token_cols],
+                    rhs=w3_words[:].bitcast(FP8X4),
+                    rhs_scale=w3_plane[:],
+                    start=True,
+                    stop=True,
+                )
+                nc.vector.scalar_tensor_tensor(
+                    out=y[:, r, :],
+                    in0=x2[:],
+                    scalar=1.0,
+                    in1=b3_row[:],
+                    op0=ALU.mult,
+                    op1=ALU.add,
+                    accum_out=y_sum[:, r : r + 1],
+                )
+
+            neg_mean = stats.tile([P, PAIR], F32, name="neg_mean")
+            nc.vector.tensor_scalar_mul(out=neg_mean[:], in0=y_sum[:], scalar1=-1.0 / E)
+            dev_sq_sum = stats.tile([P, PAIR], F32, name="dev_sq_sum")
+            for r in range(PAIR):
+                dev_sq = work.tile([P, E], BF16, name="dev_sq")
+                nc.scalar.activation(
+                    out=dev_sq[:],
+                    in_=y[:, r, :],
+                    func=ACT.Square,
+                    bias=neg_mean[:, r : r + 1],
+                    accum_out=dev_sq_sum[:, r : r + 1],
+                )
+            std = stats.tile([P, PAIR], F32, name="std")
+            nc.scalar.activation(
+                out=std[:], in_=dev_sq_sum[:], func=ACT.Sqrt, scale=1.0 / E, bias=eps[:]
+            )
+            gain = stats.tile([P, PAIR], F32, name="gain")
+            nc.vector.reciprocal(out=gain[:], in_=std[:])
+            nc.vector.tensor_tensor(
+                out=gain[:], in0=gain[:], in1=mask[:, first : first + PAIR], op=ALU.mult
+            )
+            shift = stats.tile([P, PAIR], F32, name="shift")
+            nc.vector.tensor_tensor(out=shift[:], in0=neg_mean[:], in1=gain[:], op=ALU.mult)
+
+            normed = work.tile([P, PAIR, E], F32, name="normed")
+            for r in range(PAIR):
+                nc.scalar.activation(
+                    out=normed[:, r, :],
+                    in_=y[:, r, :],
+                    func=ACT.Identity,
+                    scale=gain[:, r : r + 1],
+                    bias=shift[:, r : r + 1],
+                )
+            scaled = work.tile([P, PAIR, E], F32, name="scaled")
+            nc.vector.tensor_tensor(
+                out=scaled[:],
+                in0=normed[:],
+                in1=g_row[:].unsqueeze(1).to_broadcast([P, PAIR, E]),
+                op=ALU.mult,
+            )
+            result = work.tile([P, PAIR, E], F32, name="result")
+            for r in range(PAIR):
+                nc.vector.scalar_tensor_tensor(
+                    out=result[:, r, :],
+                    in0=beta_row[:],
+                    scalar=mask[:, first + r : first + r + 1],
+                    in1=scaled[:, r, :],
+                    op0=ALU.mult,
+                    op1=ALU.add,
+                )
+            nc.sync.dma_start(out=out_rows[:, first : first + PAIR, :], in_=result[:])

@@ -16,7 +16,9 @@ E = 512
 TOKENS = 2 * 64 * 64
 TILES = TOKENS // P
 PAIR = 2
+PAIRS = TILES // PAIR
 TILES_PER_LOAD = 8
+LOADS = TILES // TILES_PER_LOAD
 EPS = 1e-5
 
 FLOPS = 2 * 2 * TOKENS * E * E
@@ -60,9 +62,9 @@ def tile_edgefeaturenet_pb_t_kernel(
     mask_rows = edge_mask.rearrange("b r c -> (b r c)").rearrange("(p i) -> p i", i=TILES)
 
     with tc.tile_pool(name="keep", bufs=1) as keep, tc.tile_pool(
-        name="loads", bufs=3
-    ) as loads, tc.tile_pool(name="work", bufs=3) as work, tc.tile_pool(
-        name="stats", bufs=4
+        name="work", bufs=2
+    ) as work, tc.tile_pool(name="rows", bufs=3) as rows, tc.tile_pool(
+        name="stats", bufs=3
     ) as stats, tc.psum_pool(name="psum_t", bufs=1) as psum_t, tc.psum_pool(
         name="psum_x", bufs=3
     ) as psum_x, tc.psum_pool(name="psum_y", bufs=3) as psum_y:
@@ -71,17 +73,27 @@ def tile_edgefeaturenet_pb_t_kernel(
         warm = keep.tile([P, 1], F32, name="warm")
         nc.scalar.activation(out=warm[:], in_=eps[:], func=ACT.Sqrt)
 
+        h1_sb = []
+        for g in range(LOADS):
+            h1_sb.append(keep.tile([P, TILES_PER_LOAD, E], BF16, name="h1_sb%d" % g))
+
+        def load_h1(g):
+            nc.sync.dma_start(
+                out=h1_sb[g][:],
+                in_=h1_rows[:, g * TILES_PER_LOAD : (g + 1) * TILES_PER_LOAD, :],
+            )
+
+        load_h1(0)
         w2_words, w2_plane = load_weight(nc, keep, W2_words, W2_scales, "w2")
         b2_row = load_row_to_all_partitions(nc, keep, b2, "b2_row")
         w3_words, w3_plane = load_weight(nc, keep, W3_words, W3_scales, "w3")
+        for g in range(1, LOADS):
+            load_h1(g)
         b3_row = load_row_to_all_partitions(nc, keep, b3, "b3_row")
-        g_row = load_row_to_all_partitions(nc, keep, ln_g, "g_row")
-        beta_row = load_row_to_all_partitions(nc, keep, ln_b, "beta_row")
-
         mask_bf = keep.tile([P, TILES], BF16, name="mask_bf")
         nc.scalar.dma_start(out=mask_bf[:], in_=mask_rows)
-        mask = keep.tile([P, TILES], F32, name="mask")
-        nc.vector.tensor_copy(out=mask[:], in_=mask_bf[:])
+        g_bf = load_row_to_all_partitions(nc, keep, ln_g, "g_bf")
+        beta_row = load_row_to_all_partitions(nc, keep, ln_b, "beta_row")
 
         ident_f32 = keep.tile([P, P], F32, name="ident_f32")
         make_identity(nc, ident_f32[:])
@@ -92,130 +104,187 @@ def tile_edgefeaturenet_pb_t_kernel(
         nc.vector.tensor_copy(
             out=b2_sorted[:], in_=b2_row[:].rearrange("p (m t) -> p t m", t=PACK)
         )
+        mask = keep.tile([P, TILES], F32, name="mask")
+        nc.vector.tensor_copy(out=mask[:], in_=mask_bf[:])
+        g_row = keep.tile([P, E], F32, name="g_row")
+        nc.vector.tensor_copy(out=g_row[:], in_=g_bf[:])
 
-        for first in range(0, TILES, PAIR):
-            if first % TILES_PER_LOAD == 0:
-                h1_sb = loads.tile([P, TILES_PER_LOAD, E], BF16, name="h1_sb")
-                nc.sync.dma_start(
-                    out=h1_sb[:], in_=h1_rows[:, first : first + TILES_PER_LOAD, :]
-                )
+        tiles = {}
 
+        def transpose_h1(j):
             h1T = psum_t.tile([P, PAIR, 2, P], F32, name="h1T")
             for r in range(PAIR):
-                words = h1_sb[:, first % TILES_PER_LOAD + r, :].bitcast(F32)
+                i = PAIR * j + r
+                words = h1_sb[i // TILES_PER_LOAD][:, i % TILES_PER_LOAD, :].bitcast(F32)
                 for u in range(2):
                     nc.tensor.transpose(h1T[:, r, u, :], words[:, u : E // 2 : 2], ident_f32[:])
-            h1_grouped = work.tile([P, PAIR * P * PACK], BF16, name="h1_grouped", align_bytes=64)
-            nc.scalar.copy(
-                out=h1_grouped[:].bitcast(F32).rearrange("p (r w u) -> p r w u", r=PAIR, u=2),
-                in_=h1T[:].rearrange("p r u w -> p r w u"),
-            )
-            h1_codes, h1_scales = quantise_pair(nc, work, h1_grouped, "h1")
+            tiles["h1T", j] = h1T
 
-            h_sorted = work.tile([P, PAIR, PACK, P], BF16, name="h_sorted")
+        def group_h1(j):
+            grouped = work.tile([P, PAIR * P * PACK], BF16, name="h1_grouped", align_bytes=64)
+            nc.scalar.copy(
+                out=grouped[:].bitcast(F32).rearrange("p (r w u) -> p r w u", r=PAIR, u=2),
+                in_=tiles["h1T", j][:].rearrange("p r u w -> p r w u"),
+            )
+            tiles["h1_grouped", j] = grouped
+
+        def quantise_h1(j):
+            tiles["h1_mx", j] = quantise_pair(nc, work, tiles["h1_grouped", j], "h1")
+
+        def mx_layer(j, operand, weight_words, weight_plane, pool, name):
+            codes, scales = tiles[operand, j]
             for r in range(PAIR):
                 token_cols = slice(r * P, (r + 1) * P)
-                x1 = psum_x.tile([P, E], F32, name="x1")
+                product = pool.tile([P, E], F32, name=name)
                 nc.tensor.matmul_mx(
-                    out=x1[:],
-                    lhsT=h1_codes[:, token_cols].bitcast(FP8X4),
-                    lhsT_scale=h1_scales[:, token_cols],
-                    rhs=w2_words[:].bitcast(FP8X4),
-                    rhs_scale=w2_plane[:],
+                    out=product[:],
+                    lhsT=codes[:, token_cols].bitcast(FP8X4),
+                    lhsT_scale=scales[:, token_cols],
+                    rhs=weight_words[:].bitcast(FP8X4),
+                    rhs_scale=weight_plane[:],
                     start=True,
                     stop=True,
                 )
+                tiles[name, j, r] = product
+
+        def layer1(j):
+            mx_layer(j, "h1_mx", w2_words, w2_plane, psum_x, "x1")
+
+        def add_b2(j):
+            h_sorted = work.tile([P, PAIR, PACK, P], BF16, name="h_sorted")
+            for r in range(PAIR):
                 nc.vector.tensor_tensor(
                     out=h_sorted[:, r, :, :],
-                    in0=x1[:].rearrange("p (m t) -> p t m", t=PACK),
+                    in0=tiles["x1", j, r][:].rearrange("p (m t) -> p t m", t=PACK),
                     in1=b2_sorted[:],
                     op=ALU.add,
                 )
+            tiles["h_sorted", j] = h_sorted
 
+        def transpose_h(j):
             hT = psum_t.tile([P, PAIR, PACK, P], BF16, name="hT")
             for r in range(PAIR):
                 for t in range(PACK):
-                    nc.tensor.transpose(hT[:, r, t, :], h_sorted[:, r, t, :], ident_bf[:])
-            h_grouped = work.tile([P, PAIR * P * PACK], BF16, name="h_grouped", align_bytes=64)
+                    nc.tensor.transpose(
+                        hT[:, r, t, :], tiles["h_sorted", j][:, r, t, :], ident_bf[:]
+                    )
+            tiles["hT", j] = hT
+
+        def group_h(j):
+            grouped = work.tile([P, PAIR * P * PACK], BF16, name="h_grouped", align_bytes=64)
             nc.scalar.activation(
-                out=h_grouped[:].rearrange("p (r w t) -> p r w t", r=PAIR, t=PACK),
-                in_=hT[:].rearrange("p r t w -> p r w t"),
+                out=grouped[:].rearrange("p (r w t) -> p r w t", r=PAIR, t=PACK),
+                in_=tiles["hT", j][:].rearrange("p r t w -> p r w t"),
                 func=ACT.Relu,
             )
-            h_codes, h_scales = quantise_pair(nc, work, h_grouped, "h")
+            tiles["h_grouped", j] = grouped
 
-            y = work.tile([P, PAIR, E], F32, name="y")
+        def quantise_h(j):
+            tiles["h_mx", j] = quantise_pair(nc, work, tiles["h_grouped", j], "h")
+
+        def layer2(j):
+            mx_layer(j, "h_mx", w3_words, w3_plane, psum_y, "x2")
+
+        def add_b3(j):
+            y = rows.tile([P, PAIR, E], F32, name="y")
             y_sum = stats.tile([P, PAIR], F32, name="y_sum")
             for r in range(PAIR):
-                token_cols = slice(r * P, (r + 1) * P)
-                x2 = psum_y.tile([P, E], F32, name="x2")
-                nc.tensor.matmul_mx(
-                    out=x2[:],
-                    lhsT=h_codes[:, token_cols].bitcast(FP8X4),
-                    lhsT_scale=h_scales[:, token_cols],
-                    rhs=w3_words[:].bitcast(FP8X4),
-                    rhs_scale=w3_plane[:],
-                    start=True,
-                    stop=True,
-                )
                 nc.vector.scalar_tensor_tensor(
                     out=y[:, r, :],
-                    in0=x2[:],
+                    in0=tiles["x2", j, r][:],
                     scalar=1.0,
                     in1=b3_row[:],
                     op0=ALU.mult,
                     op1=ALU.add,
                     accum_out=y_sum[:, r : r + 1],
                 )
-
             neg_mean = stats.tile([P, PAIR], F32, name="neg_mean")
             nc.vector.tensor_scalar_mul(out=neg_mean[:], in0=y_sum[:], scalar1=-1.0 / E)
+            tiles["y", j] = y
+            tiles["neg_mean", j] = neg_mean
+
+        def deviations(j):
             dev_sq_sum = stats.tile([P, PAIR], F32, name="dev_sq_sum")
             for r in range(PAIR):
                 dev_sq = work.tile([P, E], BF16, name="dev_sq")
                 nc.scalar.activation(
                     out=dev_sq[:],
-                    in_=y[:, r, :],
+                    in_=tiles["y", j][:, r, :],
                     func=ACT.Square,
-                    bias=neg_mean[:, r : r + 1],
+                    bias=tiles["neg_mean", j][:, r : r + 1],
                     accum_out=dev_sq_sum[:, r : r + 1],
                 )
             std = stats.tile([P, PAIR], F32, name="std")
             nc.scalar.activation(
                 out=std[:], in_=dev_sq_sum[:], func=ACT.Sqrt, scale=1.0 / E, bias=eps[:]
             )
+            tiles["std", j] = std
+
+        def gains(j):
             gain = stats.tile([P, PAIR], F32, name="gain")
-            nc.vector.reciprocal(out=gain[:], in_=std[:])
+            nc.vector.reciprocal(out=gain[:], in_=tiles["std", j][:])
             nc.vector.tensor_tensor(
-                out=gain[:], in0=gain[:], in1=mask[:, first : first + PAIR], op=ALU.mult
+                out=gain[:], in0=gain[:], in1=mask[:, PAIR * j : PAIR * (j + 1)], op=ALU.mult
             )
             shift = stats.tile([P, PAIR], F32, name="shift")
-            nc.vector.tensor_tensor(out=shift[:], in0=neg_mean[:], in1=gain[:], op=ALU.mult)
+            nc.vector.tensor_tensor(
+                out=shift[:], in0=tiles["neg_mean", j][:], in1=gain[:], op=ALU.mult
+            )
+            tiles["gain", j] = gain
+            tiles["shift", j] = shift
 
-            normed = work.tile([P, PAIR, E], F32, name="normed")
+        def normalise(j):
+            normed = rows.tile([P, PAIR, E], F32, name="normed")
             for r in range(PAIR):
                 nc.scalar.activation(
                     out=normed[:, r, :],
-                    in_=y[:, r, :],
+                    in_=tiles["y", j][:, r, :],
                     func=ACT.Identity,
-                    scale=gain[:, r : r + 1],
-                    bias=shift[:, r : r + 1],
+                    scale=tiles["gain", j][:, r : r + 1],
+                    bias=tiles["shift", j][:, r : r + 1],
                 )
-            scaled = work.tile([P, PAIR, E], F32, name="scaled")
-            nc.vector.tensor_tensor(
-                out=scaled[:],
-                in0=normed[:],
-                in1=g_row[:].unsqueeze(1).to_broadcast([P, PAIR, E]),
-                op=ALU.mult,
-            )
-            result = work.tile([P, PAIR, E], F32, name="result")
+            tiles["normed", j] = normed
+
+        def scale_by_g(j):
+            scaled = rows.tile([P, PAIR, E], F32, name="scaled")
             for r in range(PAIR):
+                nc.gpsimd.tensor_tensor(
+                    out=scaled[:, r, :], in0=tiles["normed", j][:, r, :], in1=g_row[:], op=ALU.mult
+                )
+            tiles["scaled", j] = scaled
+
+        def finish(j):
+            result = rows.tile([P, PAIR, E], F32, name="result")
+            for r in range(PAIR):
+                i = PAIR * j + r
                 nc.vector.scalar_tensor_tensor(
                     out=result[:, r, :],
                     in0=beta_row[:],
-                    scalar=mask[:, first + r : first + r + 1],
-                    in1=scaled[:, r, :],
+                    scalar=mask[:, i : i + 1],
+                    in1=tiles["scaled", j][:, r, :],
                     op0=ALU.mult,
                     op1=ALU.add,
                 )
-            nc.sync.dma_start(out=out_rows[:, first : first + PAIR, :], in_=result[:])
+            nc.sync.dma_start(out=out_rows[:, PAIR * j : PAIR * (j + 1), :], in_=result[:])
+
+        def run(stage, j):
+            if 0 <= j < PAIRS:
+                stage(j)
+
+        with tc.manual_schedule():
+            for n in range(-1, PAIRS + 3):
+                run(transpose_h1, n + 1)
+                run(quantise_h1, n)
+                run(layer1, n)
+                run(quantise_h, n - 1)
+                run(layer2, n - 1)
+                run(deviations, n - 2)
+                run(finish, n - 3)
+                run(group_h1, n + 1)
+                run(gains, n - 2)
+                run(normalise, n - 2)
+                run(scale_by_g, n - 2)
+                run(add_b2, n)
+                run(transpose_h, n)
+                run(add_b3, n - 1)
+                run(group_h, n)

@@ -71,7 +71,7 @@ def tile_edgefeaturenet_pb_t_kernel(
         eps = keep.tile([P, 1], F32, name="eps")
         nc.vector.memset(eps[:], EPS)
         warm = keep.tile([P, 1], F32, name="warm")
-        nc.scalar.activation(out=warm[:], in_=eps[:], func=ACT.Sqrt)
+        nc.scalar.activation(out=warm[:], in_=eps[:], func=ACT.Abs_reciprocal_sqrt)
 
         h1_sb = []
         for g in range(LOADS):
@@ -198,12 +198,12 @@ def tile_edgefeaturenet_pb_t_kernel(
                     op1=ALU.add,
                     accum_out=y_sum[:, r : r + 1],
                 )
-            neg_mean = stats.tile([P, PAIR], F32, name="neg_mean")
-            nc.vector.tensor_scalar_mul(out=neg_mean[:], in0=y_sum[:], scalar1=-1.0 / E)
             tiles["y", j] = y
-            tiles["neg_mean", j] = neg_mean
+            tiles["y_sum", j] = y_sum
 
         def deviations(j):
+            neg_mean = stats.tile([P, PAIR], F32, name="neg_mean")
+            nc.scalar.mul(out=neg_mean[:], in_=tiles["y_sum", j][:], mul=-1.0 / E)
             dev_sq_sum = stats.tile([P, PAIR], F32, name="dev_sq_sum")
             for r in range(PAIR):
                 dev_sq = work.tile([P, E], BF16, name="dev_sq")
@@ -211,37 +211,40 @@ def tile_edgefeaturenet_pb_t_kernel(
                     out=dev_sq[:],
                     in_=tiles["y", j][:, r, :],
                     func=ACT.Square,
-                    bias=tiles["neg_mean", j][:, r : r + 1],
+                    bias=neg_mean[:, r : r + 1],
                     accum_out=dev_sq_sum[:, r : r + 1],
                 )
-            std = stats.tile([P, PAIR], F32, name="std")
+            rstd = stats.tile([P, PAIR], F32, name="rstd")
             nc.scalar.activation(
-                out=std[:], in_=dev_sq_sum[:], func=ACT.Sqrt, scale=1.0 / E, bias=eps[:]
+                out=rstd[:],
+                in_=dev_sq_sum[:],
+                func=ACT.Abs_reciprocal_sqrt,
+                scale=1.0 / E,
+                bias=eps[:],
             )
-            tiles["std", j] = std
+            tiles["neg_mean", j] = neg_mean
+            tiles["rstd", j] = rstd
 
         def gains(j):
             gain = stats.tile([P, PAIR], F32, name="gain")
-            nc.vector.reciprocal(out=gain[:], in_=tiles["std", j][:])
             nc.vector.tensor_tensor(
-                out=gain[:], in0=gain[:], in1=mask[:, PAIR * j : PAIR * (j + 1)], op=ALU.mult
-            )
-            shift = stats.tile([P, PAIR], F32, name="shift")
-            nc.vector.tensor_tensor(
-                out=shift[:], in0=tiles["neg_mean", j][:], in1=gain[:], op=ALU.mult
+                out=gain[:],
+                in0=tiles["rstd", j][:],
+                in1=mask[:, PAIR * j : PAIR * (j + 1)],
+                op=ALU.mult,
             )
             tiles["gain", j] = gain
-            tiles["shift", j] = shift
 
         def normalise(j):
             normed = rows.tile([P, PAIR, E], F32, name="normed")
             for r in range(PAIR):
-                nc.scalar.activation(
+                nc.vector.tensor_scalar(
                     out=normed[:, r, :],
-                    in_=tiles["y", j][:, r, :],
-                    func=ACT.Identity,
-                    scale=tiles["gain", j][:, r : r + 1],
-                    bias=tiles["shift", j][:, r : r + 1],
+                    in0=tiles["y", j][:, r, :],
+                    scalar1=tiles["neg_mean", j][:, r : r + 1],
+                    scalar2=tiles["gain", j][:, r : r + 1],
+                    op0=ALU.add,
+                    op1=ALU.mult,
                 )
             tiles["normed", j] = normed
 
@@ -253,38 +256,47 @@ def tile_edgefeaturenet_pb_t_kernel(
                 )
             tiles["scaled", j] = scaled
 
-        def finish(j):
-            result = rows.tile([P, PAIR, E], F32, name="result")
-            for r in range(PAIR):
-                i = PAIR * j + r
-                nc.vector.scalar_tensor_tensor(
-                    out=result[:, r, :],
-                    in0=beta_row[:],
-                    scalar=mask[:, i : i + 1],
-                    in1=tiles["scaled", j][:, r, :],
-                    op0=ALU.mult,
-                    op1=ALU.add,
-                )
-            nc.sync.dma_start(out=out_rows[:, PAIR * j : PAIR * (j + 1), :], in_=result[:])
+        def add_beta(j, r):
+            if r == 0:
+                tiles["result", j] = rows.tile([P, PAIR, E], F32, name="result")
+            i = PAIR * j + r
+            nc.vector.scalar_tensor_tensor(
+                out=tiles["result", j][:, r, :],
+                in0=beta_row[:],
+                scalar=mask[:, i : i + 1],
+                in1=tiles["scaled", j][:, r, :],
+                op0=ALU.mult,
+                op1=ALU.add,
+            )
+
+        def add_beta_first(j):
+            add_beta(j, 0)
+
+        def add_beta_second_and_store(j):
+            add_beta(j, 1)
+            nc.sync.dma_start(
+                out=out_rows[:, PAIR * j : PAIR * (j + 1), :], in_=tiles["result", j][:]
+            )
 
         def run(stage, j):
             if 0 <= j < PAIRS:
                 stage(j)
 
         with tc.manual_schedule():
-            for n in range(-1, PAIRS + 3):
-                run(transpose_h1, n + 1)
-                run(quantise_h1, n)
-                run(layer1, n)
-                run(quantise_h, n - 1)
-                run(layer2, n - 1)
+            for n in range(-2, PAIRS + 3):
+                run(transpose_h1, n + 2)
+                run(add_b3, n - 2)
                 run(deviations, n - 2)
-                run(finish, n - 3)
-                run(group_h1, n + 1)
-                run(gains, n - 2)
-                run(normalise, n - 2)
-                run(scale_by_g, n - 2)
                 run(add_b2, n)
                 run(transpose_h, n)
-                run(add_b3, n - 1)
+                run(quantise_h, n - 1)
+                run(layer2, n - 1)
+                run(quantise_h1, n + 1)
+                run(layer1, n + 1)
+                run(group_h1, n + 2)
+                run(add_beta_first, n - 3)
+                run(gains, n - 2)
+                run(add_beta_second_and_store, n - 3)
+                run(normalise, n - 2)
+                run(scale_by_g, n - 2)
                 run(group_h, n)

@@ -67,7 +67,9 @@ def tile_edgefeaturenet_pb_t_kernel(
         name="stats", bufs=3
     ) as stats, tc.psum_pool(name="psum_t", bufs=1) as psum_t, tc.psum_pool(
         name="psum_x", bufs=3
-    ) as psum_x, tc.psum_pool(name="psum_y", bufs=3) as psum_y:
+    ) as psum_x, tc.psum_pool(name="psum_y", bufs=2) as psum_y, tc.psum_pool(
+        name="psum_keep", bufs=1
+    ) as psum_keep:
         eps = keep.tile([P, 1], F32, name="eps")
         nc.vector.memset(eps[:], EPS)
         warm = keep.tile([P, 1], F32, name="warm")
@@ -99,6 +101,8 @@ def tile_edgefeaturenet_pb_t_kernel(
         make_identity(nc, ident_f32[:])
         ident_bf = keep.tile([P, P], BF16, name="ident_bf")
         make_identity(nc, ident_bf[:])
+
+        beta_psum = psum_keep.tile([P, E], F32, name="beta_psum")
 
         b2_sorted = keep.tile([P, PACK, P], BF16, name="b2_sorted")
         nc.vector.tensor_copy(
@@ -262,7 +266,7 @@ def tile_edgefeaturenet_pb_t_kernel(
             i = PAIR * j + r
             nc.vector.scalar_tensor_tensor(
                 out=tiles["result", j][:, r, :],
-                in0=beta_row[:],
+                in0=beta_psum[:],
                 scalar=mask[:, i : i + 1],
                 in1=tiles["scaled", j][:, r, :],
                 op0=ALU.mult,
@@ -283,20 +287,24 @@ def tile_edgefeaturenet_pb_t_kernel(
                 stage(j)
 
         with tc.manual_schedule():
-            for n in range(-2, PAIRS + 3):
+            for n in range(-2, PAIRS + 4):
+                if n == 2:
+                    nc.tensor.matmul(
+                        beta_psum[:], lhsT=ident_bf[:], rhs=beta_row[:], start=True, stop=True
+                    )
                 run(transpose_h1, n + 2)
                 run(add_b3, n - 2)
                 run(deviations, n - 2)
                 run(add_b2, n)
                 run(transpose_h, n)
+                run(add_beta_first, n - 4)
+                run(add_beta_second_and_store, n - 4)
                 run(quantise_h, n - 1)
                 run(layer2, n - 1)
                 run(quantise_h1, n + 1)
                 run(layer1, n + 1)
                 run(group_h1, n + 2)
-                run(add_beta_first, n - 3)
                 run(gains, n - 2)
-                run(add_beta_second_and_store, n - 3)
                 run(normalise, n - 2)
                 run(scale_by_g, n - 2)
                 run(group_h, n)

@@ -17,8 +17,8 @@ TOKENS = 2 * 64 * 64
 TILES = TOKENS // P
 PAIR = 2
 PAIRS = TILES // PAIR
-TILES_PER_LOAD = 8
-LOADS = TILES // TILES_PER_LOAD
+QUAD = 4
+QUADS = TILES // QUAD
 EPS = 1e-5
 
 FLOPS = 2 * 2 * TOKENS * E * E
@@ -46,9 +46,9 @@ def load_row_to_all_partitions(nc, keep, vector_dram, name):
     return row
 
 
-def quantise_pair(nc, pool, grouped, name):
-    codes = pool.tile([P, PAIR * P], U32, name=name + "_codes", align_bytes=64)
-    scales = pool.tile([P, PAIR * P], U8, name=name + "_scales", align_bytes=64)
+def quantise_quad(nc, pool, grouped, name):
+    codes = pool.tile([P, QUAD * P], U32, name=name + "_codes", align_bytes=64)
+    scales = pool.tile([P, QUAD * P], U8, name=name + "_scales", align_bytes=64)
     nc.vector.quantize_mx(out=codes[:].bitcast(FP8X4), scales=scales[:], in_=grouped[:])
     return codes, scales
 
@@ -62,10 +62,10 @@ def tile_edgefeaturenet_pb_t_kernel(
     mask_rows = edge_mask.rearrange("b r c -> (b r c)").rearrange("(p i) -> p i", i=TILES)
 
     with tc.tile_pool(name="keep", bufs=1) as keep, tc.tile_pool(
-        name="work", bufs=2
-    ) as work, tc.tile_pool(name="rows", bufs=3) as rows, tc.tile_pool(
+        name="front", bufs=2
+    ) as front, tc.tile_pool(name="rows", bufs=4) as rows, tc.tile_pool(
         name="stats", bufs=3
-    ) as stats, tc.psum_pool(name="psum_t", bufs=1) as psum_t, tc.psum_pool(
+    ) as stats, tc.psum_pool(name="psum_t", bufs=2) as psum_t, tc.psum_pool(
         name="psum_x", bufs=3
     ) as psum_x, tc.psum_pool(name="psum_y", bufs=2) as psum_y, tc.psum_pool(
         name="psum_keep", bufs=1
@@ -76,21 +76,20 @@ def tile_edgefeaturenet_pb_t_kernel(
         nc.scalar.activation(out=warm[:], in_=eps[:], func=ACT.Abs_reciprocal_sqrt)
 
         h1_sb = []
-        for g in range(LOADS):
-            h1_sb.append(keep.tile([P, TILES_PER_LOAD, E], BF16, name="h1_sb%d" % g))
+        for q in range(QUADS):
+            h1_sb.append(keep.tile([P, QUAD, E], BF16, name="h1_sb%d" % q))
 
-        def load_h1(g):
-            nc.sync.dma_start(
-                out=h1_sb[g][:],
-                in_=h1_rows[:, g * TILES_PER_LOAD : (g + 1) * TILES_PER_LOAD, :],
-            )
+        def load_h1(q):
+            nc.sync.dma_start(out=h1_sb[q][:], in_=h1_rows[:, q * QUAD : (q + 1) * QUAD, :])
 
         load_h1(0)
         w2_words, w2_plane = load_weight(nc, keep, W2_words, W2_scales, "w2")
-        b2_row = load_row_to_all_partitions(nc, keep, b2, "b2_row")
+        b2_bf = keep.tile([P, PACK], BF16, name="b2_bf")
+        nc.scalar.dma_start(out=b2_bf[:], in_=b2.rearrange("(p t) -> p t", t=PACK))
+        load_h1(1)
         w3_words, w3_plane = load_weight(nc, keep, W3_words, W3_scales, "w3")
-        for g in range(1, LOADS):
-            load_h1(g)
+        for q in range(2, QUADS):
+            load_h1(q)
         b3_row = load_row_to_all_partitions(nc, keep, b3, "b3_row")
         mask_bf = keep.tile([P, TILES], BF16, name="mask_bf")
         nc.scalar.dma_start(out=mask_bf[:], in_=mask_rows)
@@ -102,209 +101,251 @@ def tile_edgefeaturenet_pb_t_kernel(
         ident_bf = keep.tile([P, P], BF16, name="ident_bf")
         make_identity(nc, ident_bf[:])
 
-        beta_psum = psum_keep.tile([P, E], F32, name="beta_psum")
-
-        b2_sorted = keep.tile([P, PACK, P], BF16, name="b2_sorted")
+        w2_sorted = keep.tile([P, E], U32, name="w2_sorted", align_bytes=64)
         nc.vector.tensor_copy(
-            out=b2_sorted[:], in_=b2_row[:].rearrange("p (m t) -> p t m", t=PACK)
+            out=w2_sorted[:].bitcast(I32).rearrange("p (t m) -> p t m", t=PACK),
+            in_=w2_words[:].bitcast(I32).rearrange("p (m t) -> p t m", t=PACK),
         )
+        w2_sorted_plane = keep.tile([P, E], U8, name="w2_sorted_plane", align_bytes=64)
+        nc.vector.tensor_copy(
+            out=w2_sorted_plane[:].rearrange("p (t m) -> p m t", t=PACK),
+            in_=w2_plane[:].rearrange("p (m t) -> p m t", t=PACK),
+        )
+        b2_cols = keep.tile([P, PACK], F32, name="b2_cols")
+        nc.vector.tensor_copy(out=b2_cols[:], in_=b2_bf[:])
         mask = keep.tile([P, TILES], F32, name="mask")
         nc.vector.tensor_copy(out=mask[:], in_=mask_bf[:])
         g_row = keep.tile([P, E], F32, name="g_row")
         nc.vector.tensor_copy(out=g_row[:], in_=g_bf[:])
+        beta_psum = psum_keep.tile([P, E], F32, name="beta_psum")
 
         tiles = {}
 
-        def transpose_h1(j):
+        def transpose_h1(k):
             h1T = psum_t.tile([P, PAIR, 2, P], F32, name="h1T")
             for r in range(PAIR):
-                i = PAIR * j + r
-                words = h1_sb[i // TILES_PER_LOAD][:, i % TILES_PER_LOAD, :].bitcast(F32)
+                i = PAIR * k + r
+                words = h1_sb[i // QUAD][:, i % QUAD, :].bitcast(F32)
                 for u in range(2):
                     nc.tensor.transpose(h1T[:, r, u, :], words[:, u : E // 2 : 2], ident_f32[:])
-            tiles["h1T", j] = h1T
+            tiles["h1T", k] = h1T
 
-        def group_h1(j):
-            grouped = work.tile([P, PAIR * P * PACK], BF16, name="h1_grouped", align_bytes=64)
+        def group_h1(k):
+            q, half = k // 2, k % 2
+            if half == 0:
+                tiles["h1_grouped", q] = front.tile(
+                    [P, QUAD * P * PACK], BF16, name="h1_grouped", align_bytes=64
+                )
+            words = tiles["h1_grouped", q][:].bitcast(F32)
             nc.scalar.copy(
-                out=grouped[:].bitcast(F32).rearrange("p (r w u) -> p r w u", r=PAIR, u=2),
-                in_=tiles["h1T", j][:].rearrange("p r u w -> p r w u"),
+                out=words[:, half * PAIR * P * 2 : (half + 1) * PAIR * P * 2].rearrange(
+                    "p (r w u) -> p r w u", r=PAIR, u=2
+                ),
+                in_=tiles["h1T", k][:].rearrange("p r u w -> p r w u"),
             )
-            tiles["h1_grouped", j] = grouped
 
-        def quantise_h1(j):
-            tiles["h1_mx", j] = quantise_pair(nc, work, tiles["h1_grouped", j], "h1")
+        def quantise_h1(q):
+            tiles["h1_mx", q] = quantise_quad(nc, front, tiles["h1_grouped", q], "h1")
 
-        def mx_layer(j, operand, weight_words, weight_plane, pool, name):
-            codes, scales = tiles[operand, j]
+        def layer1(q, t):
+            codes, scales = tiles["h1_mx", q]
+            feature_cols = slice(t * P, (t + 1) * P)
+            product = psum_x.tile([P, QUAD * P], F32, name="x1")
+            nc.tensor.matmul_mx(
+                out=product[:],
+                lhsT=w2_sorted[:, feature_cols].bitcast(FP8X4),
+                lhsT_scale=w2_sorted_plane[:, feature_cols],
+                rhs=codes[:].bitcast(FP8X4),
+                rhs_scale=scales[:],
+                start=True,
+                stop=True,
+            )
+            tiles["x1", q, t] = product
+
+        def bias_relu(q, t):
+            if t == 0:
+                tiles["h_by_t", q] = front.tile([P, PACK, QUAD * P], BF16, name="h_by_t")
+            nc.scalar.activation(
+                out=tiles["h_by_t", q][:, t, :],
+                in_=tiles["x1", q, t][:],
+                func=ACT.Relu,
+                bias=b2_cols[:, t : t + 1],
+            )
+
+        def group_h(q):
+            grouped = front.tile([P, QUAD * P * PACK], BF16, name="h_grouped", align_bytes=64)
+            nc.vector.tensor_copy(
+                out=grouped[:].rearrange("p (w t) -> p w t", t=PACK),
+                in_=tiles["h_by_t", q][:].rearrange("p t w -> p w t"),
+            )
+            tiles["h_grouped", q] = grouped
+
+        def quantise_h(q):
+            tiles["h_mx", q] = quantise_quad(nc, front, tiles["h_grouped", q], "h")
+
+        def layer2(k):
+            codes, scales = tiles["h_mx", k // 2]
             for r in range(PAIR):
-                token_cols = slice(r * P, (r + 1) * P)
-                product = pool.tile([P, E], F32, name=name)
+                first = (PAIR * (k % 2) + r) * P
+                token_cols = slice(first, first + P)
+                product = psum_y.tile([P, E], F32, name="x2")
                 nc.tensor.matmul_mx(
                     out=product[:],
                     lhsT=codes[:, token_cols].bitcast(FP8X4),
                     lhsT_scale=scales[:, token_cols],
-                    rhs=weight_words[:].bitcast(FP8X4),
-                    rhs_scale=weight_plane[:],
+                    rhs=w3_words[:].bitcast(FP8X4),
+                    rhs_scale=w3_plane[:],
                     start=True,
                     stop=True,
                 )
-                tiles[name, j, r] = product
+                tiles["x2", k, r] = product
 
-        def layer1(j):
-            mx_layer(j, "h1_mx", w2_words, w2_plane, psum_x, "x1")
-
-        def add_b2(j):
-            h_sorted = work.tile([P, PAIR, PACK, P], BF16, name="h_sorted")
-            for r in range(PAIR):
-                nc.vector.tensor_tensor(
-                    out=h_sorted[:, r, :, :],
-                    in0=tiles["x1", j, r][:].rearrange("p (m t) -> p t m", t=PACK),
-                    in1=b2_sorted[:],
-                    op=ALU.add,
-                )
-            tiles["h_sorted", j] = h_sorted
-
-        def transpose_h(j):
-            hT = psum_t.tile([P, PAIR, PACK, P], BF16, name="hT")
-            for r in range(PAIR):
-                for t in range(PACK):
-                    nc.tensor.transpose(
-                        hT[:, r, t, :], tiles["h_sorted", j][:, r, t, :], ident_bf[:]
-                    )
-            tiles["hT", j] = hT
-
-        def group_h(j):
-            grouped = work.tile([P, PAIR * P * PACK], BF16, name="h_grouped", align_bytes=64)
-            nc.scalar.activation(
-                out=grouped[:].rearrange("p (r w t) -> p r w t", r=PAIR, t=PACK),
-                in_=tiles["hT", j][:].rearrange("p r t w -> p r w t"),
-                func=ACT.Relu,
-            )
-            tiles["h_grouped", j] = grouped
-
-        def quantise_h(j):
-            tiles["h_mx", j] = quantise_pair(nc, work, tiles["h_grouped", j], "h")
-
-        def layer2(j):
-            mx_layer(j, "h_mx", w3_words, w3_plane, psum_y, "x2")
-
-        def add_b3(j):
+        def add_b3(k):
+            q, half = k // 2, k % 2
+            if half == 0:
+                tiles["y_sum", q] = stats.tile([P, QUAD], F32, name="y_sum")
             y = rows.tile([P, PAIR, E], F32, name="y")
-            y_sum = stats.tile([P, PAIR], F32, name="y_sum")
             for r in range(PAIR):
+                c = PAIR * half + r
                 nc.vector.scalar_tensor_tensor(
                     out=y[:, r, :],
-                    in0=tiles["x2", j, r][:],
+                    in0=tiles["x2", k, r][:],
                     scalar=1.0,
                     in1=b3_row[:],
                     op0=ALU.mult,
                     op1=ALU.add,
-                    accum_out=y_sum[:, r : r + 1],
+                    accum_out=tiles["y_sum", q][:, c : c + 1],
                 )
-            tiles["y", j] = y
-            tiles["y_sum", j] = y_sum
+            tiles["y", k] = y
 
-        def deviations(j):
-            neg_mean = stats.tile([P, PAIR], F32, name="neg_mean")
-            nc.scalar.mul(out=neg_mean[:], in_=tiles["y_sum", j][:], mul=-1.0 / E)
-            dev_sq_sum = stats.tile([P, PAIR], F32, name="dev_sq_sum")
+        def deviations(k):
+            q, half = k // 2, k % 2
+            if half == 0:
+                tiles["dev_sq_sum", q] = stats.tile([P, QUAD], F32, name="dev_sq_sum")
             for r in range(PAIR):
-                dev_sq = work.tile([P, E], BF16, name="dev_sq")
+                c = PAIR * half + r
+                dev_sq = front.tile([P, E], BF16, name="dev_sq")
                 nc.scalar.activation(
                     out=dev_sq[:],
-                    in_=tiles["y", j][:, r, :],
+                    in_=tiles["y", k][:, r, :],
                     func=ACT.Square,
-                    bias=neg_mean[:, r : r + 1],
-                    accum_out=dev_sq_sum[:, r : r + 1],
+                    scale=-1.0 * E,
+                    bias=tiles["y_sum", q][:, c : c + 1],
+                    accum_out=tiles["dev_sq_sum", q][:, c : c + 1],
                 )
-            rstd = stats.tile([P, PAIR], F32, name="rstd")
+
+        def reciprocal_std(q):
+            rstd = stats.tile([P, QUAD], F32, name="rstd")
             nc.scalar.activation(
                 out=rstd[:],
-                in_=dev_sq_sum[:],
+                in_=tiles["dev_sq_sum", q][:],
                 func=ACT.Abs_reciprocal_sqrt,
-                scale=1.0 / E,
+                scale=1.0 / (E * E * E),
                 bias=eps[:],
             )
-            tiles["neg_mean", j] = neg_mean
-            tiles["rstd", j] = rstd
+            tiles["rstd", q] = rstd
 
-        def gains(j):
-            gain = stats.tile([P, PAIR], F32, name="gain")
+        def negative_means(q):
+            neg_mean = stats.tile([P, QUAD], F32, name="neg_mean")
+            nc.vector.tensor_scalar(
+                out=neg_mean[:], in0=tiles["y_sum", q][:], scalar1=-1.0 / E, scalar2=0.0, op0=ALU.mult, op1=ALU.add,
+            )
+            tiles["neg_mean", q] = neg_mean
+
+        def gains(q):
+            gain = stats.tile([P, QUAD], F32, name="gain")
             nc.vector.tensor_tensor(
                 out=gain[:],
-                in0=tiles["rstd", j][:],
-                in1=mask[:, PAIR * j : PAIR * (j + 1)],
+                in0=tiles["rstd", q][:],
+                in1=mask[:, QUAD * q : QUAD * (q + 1)],
                 op=ALU.mult,
             )
-            tiles["gain", j] = gain
+            tiles["gain", q] = gain
 
-        def normalise(j):
+        def normalise(k):
+            q, half = k // 2, k % 2
             normed = rows.tile([P, PAIR, E], F32, name="normed")
             for r in range(PAIR):
+                c = PAIR * half + r
                 nc.vector.tensor_scalar(
                     out=normed[:, r, :],
-                    in0=tiles["y", j][:, r, :],
-                    scalar1=tiles["neg_mean", j][:, r : r + 1],
-                    scalar2=tiles["gain", j][:, r : r + 1],
+                    in0=tiles["y", k][:, r, :],
+                    scalar1=tiles["neg_mean", q][:, c : c + 1],
+                    scalar2=tiles["gain", q][:, c : c + 1],
                     op0=ALU.add,
                     op1=ALU.mult,
                 )
-            tiles["normed", j] = normed
+            tiles["normed", k] = normed
 
-        def scale_by_g(j):
+        def scale_by_g(k):
             scaled = rows.tile([P, PAIR, E], F32, name="scaled")
             for r in range(PAIR):
                 nc.gpsimd.tensor_tensor(
-                    out=scaled[:, r, :], in0=tiles["normed", j][:, r, :], in1=g_row[:], op=ALU.mult
+                    out=scaled[:, r, :], in0=tiles["normed", k][:, r, :], in1=g_row[:], op=ALU.mult
                 )
-            tiles["scaled", j] = scaled
+            tiles["scaled", k] = scaled
 
-        def add_beta(j, r):
+        def add_beta(k, r):
             if r == 0:
-                tiles["result", j] = rows.tile([P, PAIR, E], F32, name="result")
-            i = PAIR * j + r
+                tiles["result", k] = rows.tile([P, PAIR, E], F32, name="result")
+            i = PAIR * k + r
             nc.vector.scalar_tensor_tensor(
-                out=tiles["result", j][:, r, :],
+                out=tiles["result", k][:, r, :],
                 in0=beta_psum[:],
                 scalar=mask[:, i : i + 1],
-                in1=tiles["scaled", j][:, r, :],
+                in1=tiles["scaled", k][:, r, :],
                 op0=ALU.mult,
                 op1=ALU.add,
             )
 
-        def add_beta_first(j):
-            add_beta(j, 0)
+        def add_beta_first(k):
+            add_beta(k, 0)
 
-        def add_beta_second_and_store(j):
-            add_beta(j, 1)
+        def add_beta_second_and_store(k):
+            add_beta(k, 1)
             nc.sync.dma_start(
-                out=out_rows[:, PAIR * j : PAIR * (j + 1), :], in_=tiles["result", j][:]
+                out=out_rows[:, PAIR * k : PAIR * (k + 1), :], in_=tiles["result", k][:]
             )
 
-        def run(stage, j):
-            if 0 <= j < PAIRS:
-                stage(j)
+        def pair(stage, k):
+            if 0 <= k < PAIRS:
+                stage(k)
+
+        def quad(stage, q, *more):
+            if 0 <= q < QUADS:
+                stage(q, *more)
 
         with tc.manual_schedule():
-            for n in range(-2, PAIRS + 4):
-                if n == 2:
+            for k in range(-6, PAIRS + 5):
+                if k == 2:
                     nc.tensor.matmul(
                         beta_psum[:], lhsT=ident_bf[:], rhs=beta_row[:], start=True, stop=True
                     )
-                run(transpose_h1, n + 2)
-                run(add_b3, n - 2)
-                run(deviations, n - 2)
-                run(add_b2, n)
-                run(transpose_h, n)
-                run(add_beta_first, n - 4)
-                run(add_beta_second_and_store, n - 4)
-                run(quantise_h, n - 1)
-                run(layer2, n - 1)
-                run(quantise_h1, n + 1)
-                run(layer1, n + 1)
-                run(group_h1, n + 2)
-                run(gains, n - 2)
-                run(normalise, n - 2)
-                run(scale_by_g, n - 2)
-                run(group_h, n)
+                pair(add_b3, k)
+                pair(layer2, k + 1)
+                if k % 2 == 0:
+                    pair(group_h1, k + 4)
+                    pair(transpose_h1, k + 6)
+                    pair(group_h1, k + 5)
+                    pair(transpose_h1, k + 7)
+                    pair(add_beta_first, k - 4)
+                    pair(add_beta_second_and_store, k - 4)
+                    quad(group_h, (k + 2) // 2)
+                    quad(gains, (k - 2) // 2)
+                    quad(quantise_h1, (k + 4) // 2)
+                    for t in range(PACK - 1):
+                        quad(layer1, (k + 4) // 2, t)
+                    quad(quantise_h, (k + 2) // 2)
+                else:
+                    pair(deviations, k - 1)
+                    pair(deviations, k)
+                    quad(reciprocal_std, (k - 1) // 2)
+                    pair(add_beta_first, k - 4)
+                    quad(negative_means, (k - 1) // 2)
+                    pair(add_beta_second_and_store, k - 4)
+                    quad(bias_relu, (k + 3) // 2, 0)
+                    quad(layer1, (k + 3) // 2, PACK - 1)
+                    for t in range(1, PACK):
+                        quad(bias_relu, (k + 3) // 2, t)
+                pair(normalise, k - 2)
+                pair(scale_by_g, k - 2)

@@ -331,6 +331,7 @@ def tile_edgefeaturenet_pb_t_kernel(
                     pair(add_beta_first, k - 4)
                     pair(add_beta_second_and_store, k - 4)
                     quad(group_h, (k + 2) // 2)
+                    quad(negative_means, (k - 2) // 2)
                     quad(gains, (k - 2) // 2)
                     quad(quantise_h1, (k + 4) // 2)
                     for t in range(PACK - 1):
@@ -341,7 +342,6 @@ def tile_edgefeaturenet_pb_t_kernel(
                     pair(deviations, k)
                     quad(reciprocal_std, (k - 1) // 2)
                     pair(add_beta_first, k - 4)
-                    quad(negative_means, (k - 1) // 2)
                     pair(add_beta_second_and_store, k - 4)
                     quad(bias_relu, (k + 3) // 2, 0)
                     quad(layer1, (k + 3) // 2, PACK - 1)

@@ -265,17 +265,28 @@ def tile_edgefeaturenet_pb_t_kernel(
         def normalise(k):
             q, half = k // 2, k % 2
             normed = rows.tile([P, PAIR, E], F32, name="normed")
-            for r in range(PAIR):
-                c = PAIR * half + r
-                nc.vector.tensor_scalar(
-                    out=normed[:, r, :],
-                    in0=tiles["y", k][:, r, :],
-                    scalar1=tiles["neg_mean", q][:, c : c + 1],
-                    scalar2=tiles["gain", q][:, c : c + 1],
-                    op0=ALU.add,
-                    op1=ALU.mult,
-                )
             tiles["normed", k] = normed
+            c = PAIR * half
+            nc.vector.tensor_scalar(
+                out=normed[:, 0, :],
+                in0=tiles["y", k][:, 0, :],
+                scalar1=tiles["neg_mean", q][:, c : c + 1],
+                scalar2=tiles["gain", q][:, c : c + 1],
+                op0=ALU.add,
+                op1=ALU.mult,
+            )
+
+        def normalise_second_on_vector(k):
+            q, half = k // 2, k % 2
+            c = PAIR * half + 1
+            nc.vector.tensor_scalar(
+                out=tiles["normed", k][:, 1, :],
+                in0=tiles["y", k][:, 1, :],
+                scalar1=tiles["neg_mean", q][:, c : c + 1],
+                scalar2=tiles["gain", q][:, c : c + 1],
+                op0=ALU.add,
+                op1=ALU.mult,
+            )
 
         def scale_by_g(k):
             scaled = rows.tile([P, PAIR, E], F32, name="scaled")
@@ -328,24 +339,29 @@ def tile_edgefeaturenet_pb_t_kernel(
                     pair(transpose_h1, k + 6)
                     pair(group_h1, k + 5)
                     pair(transpose_h1, k + 7)
+                    pair(deviations, k)
                     pair(add_beta_first, k - 4)
                     pair(add_beta_second_and_store, k - 4)
-                    quad(group_h, (k + 2) // 2)
                     quad(negative_means, (k - 2) // 2)
                     quad(gains, (k - 2) // 2)
+                    quad(group_h, (k + 2) // 2)
                     quad(quantise_h1, (k + 4) // 2)
                     for t in range(PACK - 1):
                         quad(layer1, (k + 4) // 2, t)
+                    pair(normalise, k - 2)
+                    pair(normalise_second_on_vector, k - 2)
+                    pair(normalise, k - 1)
+                    pair(normalise_second_on_vector, k - 1)
                     quad(quantise_h, (k + 2) // 2)
+                    pair(scale_by_g, k - 2)
+                    pair(scale_by_g, k - 1)
                 else:
-                    pair(deviations, k - 1)
-                    pair(deviations, k)
-                    quad(reciprocal_std, (k - 1) // 2)
-                    pair(add_beta_first, k - 4)
-                    pair(add_beta_second_and_store, k - 4)
                     quad(bias_relu, (k + 3) // 2, 0)
                     quad(layer1, (k + 3) // 2, PACK - 1)
-                    for t in range(1, PACK):
-                        quad(bias_relu, (k + 3) // 2, t)
-                pair(normalise, k - 2)
-                pair(scale_by_g, k - 2)
+                    quad(bias_relu, (k + 3) // 2, 1)
+                    pair(deviations, k)
+                    quad(reciprocal_std, (k - 1) // 2)
+                    quad(bias_relu, (k + 3) // 2, 2)
+                    quad(bias_relu, (k + 3) // 2, 3)
+                    pair(add_beta_first, k - 4)
+                    pair(add_beta_second_and_store, k - 4)

@@ -262,6 +262,13 @@ def tile_edgefeaturenet_pb_t_kernel(
             )
             tiles["gain", q] = gain
 
+        def shifts(q):
+            shift = stats.tile([P, QUAD], F32, name="shift")
+            nc.vector.tensor_tensor(
+                out=shift[:], in0=tiles["neg_mean", q][:], in1=tiles["gain", q][:], op=ALU.mult
+            )
+            tiles["shift", q] = shift
+
         def normalise(k):
             q, half = k // 2, k % 2
             normed = rows.tile([P, PAIR, E], F32, name="normed")
@@ -276,16 +283,16 @@ def tile_edgefeaturenet_pb_t_kernel(
                 op1=ALU.mult,
             )
 
-        def normalise_second_on_vector(k):
+        def normalise_second(k):
             q, half = k // 2, k % 2
-            c = PAIR * half + 1
-            nc.vector.tensor_scalar(
-                out=tiles["normed", k][:, 1, :],
-                in0=tiles["y", k][:, 1, :],
-                scalar1=tiles["neg_mean", q][:, c : c + 1],
-                scalar2=tiles["gain", q][:, c : c + 1],
-                op0=ALU.add,
-                op1=ALU.mult,
+            c = PAIR * half
+            normed = tiles["normed", k]
+            nc.scalar.activation(
+                out=normed[:, 1, :],
+                in_=tiles["y", k][:, 1, :],
+                func=ACT.Identity,
+                scale=tiles["gain", q][:, c + 1 : c + 2],
+                bias=tiles["shift", q][:, c + 1 : c + 2],
             )
 
         def scale_by_g(k):
@@ -345,13 +352,14 @@ def tile_edgefeaturenet_pb_t_kernel(
                     quad(negative_means, (k - 2) // 2)
                     quad(gains, (k - 2) // 2)
                     quad(group_h, (k + 2) // 2)
+                    quad(shifts, (k - 2) // 2)
                     quad(quantise_h1, (k + 4) // 2)
                     for t in range(PACK - 1):
                         quad(layer1, (k + 4) // 2, t)
                     pair(normalise, k - 2)
-                    pair(normalise_second_on_vector, k - 2)
+                    pair(normalise_second, k - 2)
                     pair(normalise, k - 1)
-                    pair(normalise_second_on_vector, k - 1)
+                    pair(normalise_second, k - 1)
                     quad(quantise_h, (k + 2) // 2)
                     pair(scale_by_g, k - 2)
                     pair(scale_by_g, k - 1)

@@ -175,8 +175,8 @@ def tile_edgefeaturenet_pb_t_kernel(
         def group_h(q):
             grouped = front.tile([P, QUAD * P * PACK], BF16, name="h_grouped", align_bytes=64)
             nc.vector.tensor_copy(
-                out=grouped[:].rearrange("p (w t) -> p w t", t=PACK),
-                in_=tiles["h_by_t", q][:].rearrange("p t w -> p w t"),
+                out=grouped[:].rearrange("p (c i t) -> p c t i", i=4, t=PACK),
+                in_=tiles["h_by_t", q][:].rearrange("p t (c i) -> p c t i", i=4),
             )
             tiles["h_grouped", q] = grouped
 

@@ -245,13 +245,6 @@ def tile_edgefeaturenet_pb_t_kernel(
             )
             tiles["rstd", q] = rstd
 
-        def negative_means(q):
-            neg_mean = stats.tile([P, QUAD], F32, name="neg_mean")
-            nc.vector.tensor_scalar(
-                out=neg_mean[:], in0=tiles["y_sum", q][:], scalar1=-1.0 / E, scalar2=0.0, op0=ALU.mult, op1=ALU.add,
-            )
-            tiles["neg_mean", q] = neg_mean
-
         def gains(q):
             gain = stats.tile([P, QUAD], F32, name="gain")
             nc.vector.tensor_tensor(
@@ -264,36 +257,39 @@ def tile_edgefeaturenet_pb_t_kernel(
 
         def shifts(q):
             shift = stats.tile([P, QUAD], F32, name="shift")
-            nc.vector.tensor_tensor(
-                out=shift[:], in0=tiles["neg_mean", q][:], in1=tiles["gain", q][:], op=ALU.mult
+            nc.vector.scalar_tensor_tensor(
+                out=shift[:],
+                in0=tiles["y_sum", q][:],
+                scalar=-1.0 / E,
+                in1=tiles["gain", q][:],
+                op0=ALU.mult,
+                op1=ALU.mult,
             )
             tiles["shift", q] = shift
 
-        def normalise(k):
-            q, half = k // 2, k % 2
-            normed = rows.tile([P, PAIR, E], F32, name="normed")
-            tiles["normed", k] = normed
-            c = PAIR * half
-            nc.vector.tensor_scalar(
-                out=normed[:, 0, :],
-                in0=tiles["y", k][:, 0, :],
-                scalar1=tiles["neg_mean", q][:, c : c + 1],
-                scalar2=tiles["gain", q][:, c : c + 1],
-                op0=ALU.add,
-                op1=ALU.mult,
-            )
-
-        def normalise_second(k):
-            q, half = k // 2, k % 2
-            c = PAIR * half
-            normed = tiles["normed", k]
-            nc.scalar.activation(
-                out=normed[:, 1, :],
-                in_=tiles["y", k][:, 1, :],
-                func=ACT.Identity,
-                scale=tiles["gain", q][:, c + 1 : c + 2],
-                bias=tiles["shift", q][:, c + 1 : c + 2],
-            )
+        def normalise(k, r, on_vector):
+            if r == 0:
+                tiles["normed", k] = rows.tile([P, PAIR, E], F32, name="normed")
+            c = PAIR * (k % 2) + r
+            gain = tiles["gain", k // 2][:, c : c + 1]
+            shift = tiles["shift", k // 2][:, c : c + 1]
+            if on_vector:
+                nc.vector.tensor_scalar(
+                    out=tiles["normed", k][:, r, :],
+                    in0=tiles["y", k][:, r, :],
+                    scalar1=gain,
+                    scalar2=shift,
+                    op0=ALU.mult,
+                    op1=ALU.add,
+                )
+            else:
+                nc.scalar.activation(
+                    out=tiles["normed", k][:, r, :],
+                    in_=tiles["y", k][:, r, :],
+                    func=ACT.Identity,
+                    scale=gain,
+                    bias=shift,
+                )
 
         def scale_by_g(k):
             scaled = rows.tile([P, PAIR, E], F32, name="scaled")
@@ -325,9 +321,9 @@ def tile_edgefeaturenet_pb_t_kernel(
                 out=out_rows[:, PAIR * k : PAIR * (k + 1), :], in_=tiles["result", k][:]
             )
 
-        def pair(stage, k):
+        def pair(stage, k, *more):
             if 0 <= k < PAIRS:
-                stage(k)
+                stage(k, *more)
 
         def quad(stage, q, *more):
             if 0 <= q < QUADS:
@@ -349,17 +345,16 @@ def tile_edgefeaturenet_pb_t_kernel(
                     pair(deviations, k)
                     pair(add_beta_first, k - 4)
                     pair(add_beta_second_and_store, k - 4)
-                    quad(negative_means, (k - 2) // 2)
                     quad(gains, (k - 2) // 2)
                     quad(group_h, (k + 2) // 2)
                     quad(shifts, (k - 2) // 2)
                     quad(quantise_h1, (k + 4) // 2)
                     for t in range(PACK - 1):
                         quad(layer1, (k + 4) // 2, t)
-                    pair(normalise, k - 2)
-                    pair(normalise_second, k - 2)
-                    pair(normalise, k - 1)
-                    pair(normalise_second, k - 1)
+                    pair(normalise, k - 2, 0, True)
+                    pair(normalise, k - 2, 1, False)
+                    pair(normalise, k - 1, 0, False)
+                    pair(normalise, k - 1, 1, False)
                     quad(quantise_h, (k + 2) // 2)
                     pair(scale_by_g, k - 2)
                     pair(scale_by_g, k - 1)

@@ -115,8 +115,9 @@ def tile_edgefeaturenet_pb_t_kernel(
         nc.vector.tensor_copy(out=b2_cols[:], in_=b2_bf[:])
         mask = keep.tile([P, TILES], F32, name="mask")
         nc.vector.tensor_copy(out=mask[:], in_=mask_bf[:])
-        g_row = keep.tile([P, E], F32, name="g_row")
-        nc.vector.tensor_copy(out=g_row[:], in_=g_bf[:])
+        g_rows = keep.tile([P, PAIR, E], F32, name="g_rows")
+        for r in range(PAIR):
+            nc.vector.tensor_copy(out=g_rows[:, r, :], in_=g_bf[:])
         beta_psum = psum_keep.tile([P, E], F32, name="beta_psum")
 
         tiles = {}
@@ -293,10 +294,9 @@ def tile_edgefeaturenet_pb_t_kernel(
 
         def scale_by_g(k):
             scaled = rows.tile([P, PAIR, E], F32, name="scaled")
-            for r in range(PAIR):
-                nc.gpsimd.tensor_tensor(
-                    out=scaled[:, r, :], in0=tiles["normed", k][:, r, :], in1=g_row[:], op=ALU.mult
-                )
+            nc.gpsimd.tensor_tensor(
+                out=scaled[:], in0=tiles["normed", k][:], in1=g_rows[:], op=ALU.mult
+            )
             tiles["scaled", k] = scaled
 
         def add_beta(k, r):

@@ -40,12 +40,6 @@ def load_weight(nc, keep, words_dram, scales_dram, name):
     return words, plane
 
 
-def load_row_to_all_partitions(nc, keep, vector_dram, name):
-    row = keep.tile([P, E], BF16, name=name)
-    nc.scalar.dma_start(out=row[:], in_=vector_dram.partition_broadcast(P))
-    return row
-
-
 def quantise_quad(nc, pool, grouped, name):
     codes = pool.tile([P, QUAD * P], U32, name=name + "_codes", align_bytes=64)
     scales = pool.tile([P, QUAD * P], U8, name=name + "_scales", align_bytes=64)
@@ -90,16 +84,19 @@ def tile_edgefeaturenet_pb_t_kernel(
         w3_words, w3_plane = load_weight(nc, keep, W3_words, W3_scales, "w3")
         for q in range(2, QUADS):
             load_h1(q)
-        b3_row = load_row_to_all_partitions(nc, keep, b3, "b3_row")
+        vectors = keep.tile([P, 3, E], BF16, name="vectors")
+        nc.vector.memset(vectors[:].rearrange("p v n -> p (v n)").bitcast(I32), 0)
+        for v, vector_dram in enumerate((b3, ln_g, ln_b)):
+            nc.scalar.dma_start(
+                out=vectors[0:1, v, :], in_=vector_dram.rearrange("(o n) -> o n", o=1)
+            )
         mask_bf = keep.tile([P, TILES], BF16, name="mask_bf")
         nc.scalar.dma_start(out=mask_bf[:], in_=mask_rows)
-        g_bf = load_row_to_all_partitions(nc, keep, ln_g, "g_bf")
-        beta_row = load_row_to_all_partitions(nc, keep, ln_b, "beta_row")
 
         ident_f32 = keep.tile([P, P], F32, name="ident_f32")
         make_identity(nc, ident_f32[:])
-        ident_bf = keep.tile([P, P], BF16, name="ident_bf")
-        make_identity(nc, ident_bf[:])
+        ones = keep.tile([P, P], BF16, name="ones")
+        nc.gpsimd.memset(ones[:], 1.0)
 
         w2_sorted = keep.tile([P, E], U32, name="w2_sorted", align_bytes=64)
         nc.vector.tensor_copy(
@@ -116,9 +113,11 @@ def tile_edgefeaturenet_pb_t_kernel(
         mask = keep.tile([P, TILES], F32, name="mask")
         nc.vector.tensor_copy(out=mask[:], in_=mask_bf[:])
         g_rows = keep.tile([P, PAIR, E], F32, name="g_rows")
-        for r in range(PAIR):
-            nc.vector.tensor_copy(out=g_rows[:, r, :], in_=g_bf[:])
+        b3_row = keep.tile([P, E], BF16, name="b3_row")
         beta_psum = psum_keep.tile([P, E], F32, name="beta_psum")
+
+        def repeat_on_all_partitions(v, bank):
+            nc.tensor.matmul(bank[:], lhsT=ones[:], rhs=vectors[:, v, :], start=True, stop=True)
 
         tiles = {}
 
@@ -331,10 +330,15 @@ def tile_edgefeaturenet_pb_t_kernel(
 
         with tc.manual_schedule():
             for k in range(-6, PAIRS + 5):
-                if k == 2:
-                    nc.tensor.matmul(
-                        beta_psum[:], lhsT=ident_bf[:], rhs=beta_row[:], start=True, stop=True
-                    )
+                if k == -3:
+                    bank = psum_y.tile([P, E], F32, name="x2")
+                    repeat_on_all_partitions(0, bank)
+                    nc.vector.tensor_copy(out=b3_row[:], in_=bank[:])
+                    bank = psum_y.tile([P, E], F32, name="x2")
+                    repeat_on_all_partitions(1, bank)
+                    for r in range(PAIR):
+                        nc.vector.tensor_copy(out=g_rows[:, r, :], in_=bank[:])
+                    repeat_on_all_partitions(2, beta_psum)
                 pair(add_b3, k)
                 pair(layer2, k + 1)
                 if k % 2 == 0:

@@ -56,7 +56,7 @@ def tile_edgefeaturenet_pb_t_kernel(
     mask_rows = edge_mask.rearrange("b r c -> (b r c)").rearrange("(p i) -> p i", i=TILES)
 
     with tc.tile_pool(name="keep", bufs=1) as keep, tc.tile_pool(
-        name="front", bufs=2
+        name="front", bufs=3
     ) as front, tc.tile_pool(name="rows", bufs=4) as rows, tc.tile_pool(
         name="stats", bufs=3
     ) as stats, tc.psum_pool(name="psum_t", bufs=2) as psum_t, tc.psum_pool(
@@ -73,45 +73,36 @@ def tile_edgefeaturenet_pb_t_kernel(
         for q in range(QUADS):
             h1_sb.append(keep.tile([P, QUAD, E], BF16, name="h1_sb%d" % q))
 
-        def load_h1(q):
-            nc.sync.dma_start(out=h1_sb[q][:], in_=h1_rows[:, q * QUAD : (q + 1) * QUAD, :])
+        def load_h1(q, first=0, count=QUAD):
+            i = q * QUAD + first
+            nc.sync.dma_start(
+                out=h1_sb[q][:, first : first + count, :], in_=h1_rows[:, i : i + count, :]
+            )
 
-        load_h1(0)
+        load_h1(0, 0, PAIR)
+        load_h1(0, PAIR, PAIR)
         w2_words, w2_plane = load_weight(nc, keep, W2_words, W2_scales, "w2")
         b2_bf = keep.tile([P, PACK], BF16, name="b2_bf")
-        nc.scalar.dma_start(out=b2_bf[:], in_=b2.rearrange("(p t) -> p t", t=PACK))
+        nc.sync.dma_start(out=b2_bf[:], in_=b2.rearrange("(p t) -> p t", t=PACK))
         load_h1(1)
-        w3_words, w3_plane = load_weight(nc, keep, W3_words, W3_scales, "w3")
-        for q in range(2, QUADS):
-            load_h1(q)
         vectors = keep.tile([P, 3, E], BF16, name="vectors")
         nc.vector.memset(vectors[:].rearrange("p v n -> p (v n)").bitcast(I32), 0)
         for v, vector_dram in enumerate((b3, ln_g, ln_b)):
-            nc.scalar.dma_start(
+            nc.sync.dma_start(
                 out=vectors[0:1, v, :], in_=vector_dram.rearrange("(o n) -> o n", o=1)
             )
+        w3_words, w3_plane = load_weight(nc, keep, W3_words, W3_scales, "w3")
+        load_h1(2)
         mask_bf = keep.tile([P, TILES], BF16, name="mask_bf")
-        nc.scalar.dma_start(out=mask_bf[:], in_=mask_rows)
+        nc.sync.dma_start(out=mask_bf[:], in_=mask_rows)
+        for q in range(3, QUADS):
+            load_h1(q)
 
         ident_f32 = keep.tile([P, P], F32, name="ident_f32")
         make_identity(nc, ident_f32[:])
         ones = keep.tile([P, P], BF16, name="ones")
         nc.gpsimd.memset(ones[:], 1.0)
 
-        w2_sorted = keep.tile([P, E], U32, name="w2_sorted", align_bytes=64)
-        nc.vector.tensor_copy(
-            out=w2_sorted[:].bitcast(I32).rearrange("p (t m) -> p t m", t=PACK),
-            in_=w2_words[:].bitcast(I32).rearrange("p (m t) -> p t m", t=PACK),
-        )
-        w2_sorted_plane = keep.tile([P, E], U8, name="w2_sorted_plane", align_bytes=64)
-        nc.vector.tensor_copy(
-            out=w2_sorted_plane[:].rearrange("p (t m) -> p m t", t=PACK),
-            in_=w2_plane[:].rearrange("p (m t) -> p m t", t=PACK),
-        )
-        b2_cols = keep.tile([P, PACK], F32, name="b2_cols")
-        nc.vector.tensor_copy(out=b2_cols[:], in_=b2_bf[:])
-        mask = keep.tile([P, TILES], F32, name="mask")
-        nc.vector.tensor_copy(out=mask[:], in_=mask_bf[:])
         g_rows = keep.tile([P, PAIR, E], F32, name="g_rows")
         b3_row = keep.tile([P, E], BF16, name="b3_row")
         beta_psum = psum_keep.tile([P, E], F32, name="beta_psum")
@@ -130,27 +121,32 @@ def tile_edgefeaturenet_pb_t_kernel(
                     nc.tensor.transpose(h1T[:, r, u, :], words[:, u : E // 2 : 2], ident_f32[:])
             tiles["h1T", k] = h1T
 
-        def group_h1(k):
+        def group_h1(k, on_vector=False):
             q, half = k // 2, k % 2
             if half == 0:
                 tiles["h1_grouped", q] = front.tile(
                     [P, QUAD * P * PACK], BF16, name="h1_grouped", align_bytes=64
                 )
             words = tiles["h1_grouped", q][:].bitcast(F32)
-            nc.scalar.copy(
-                out=words[:, half * PAIR * P * 2 : (half + 1) * PAIR * P * 2].rearrange(
-                    "p (r w u) -> p r w u", r=PAIR, u=2
-                ),
-                in_=tiles["h1T", k][:].rearrange("p r u w -> p r w u"),
+            source = tiles["h1T", k][:].rearrange("p r u w -> p r w u")
+            target = words[:, half * PAIR * P * 2 : (half + 1) * PAIR * P * 2].rearrange(
+                "p (r w u) -> p r w u", r=PAIR, u=2
             )
+            if on_vector:
+                nc.vector.tensor_copy(out=target, in_=source)
+            else:
+                nc.scalar.copy(out=target, in_=source)
 
         def quantise_h1(q):
             tiles["h1_mx", q] = quantise_quad(nc, front, tiles["h1_grouped", q], "h1")
 
-        def layer1(q, t):
+        def layer1(q, t, spare_bank=False):
             codes, scales = tiles["h1_mx", q]
             feature_cols = slice(t * P, (t + 1) * P)
-            product = psum_x.tile([P, QUAD * P], F32, name="x1")
+            if spare_bank:
+                product = psum_y.tile([P, QUAD * P], F32, name="x2")
+            else:
+                product = psum_x.tile([P, QUAD * P], F32, name="x1")
             nc.tensor.matmul_mx(
                 out=product[:],
                 lhsT=w2_sorted[:, feature_cols].bitcast(FP8X4),
@@ -162,15 +158,25 @@ def tile_edgefeaturenet_pb_t_kernel(
             )
             tiles["x1", q, t] = product
 
-        def bias_relu(q, t):
+        def bias_relu(q, t, on_vector=False):
             if t == 0:
                 tiles["h_by_t", q] = front.tile([P, PACK, QUAD * P], BF16, name="h_by_t")
-            nc.scalar.activation(
-                out=tiles["h_by_t", q][:, t, :],
-                in_=tiles["x1", q, t][:],
-                func=ACT.Relu,
-                bias=b2_cols[:, t : t + 1],
-            )
+            if on_vector:
+                nc.vector.tensor_scalar(
+                    out=tiles["h_by_t", q][:, t, :],
+                    in0=tiles["x1", q, t][:],
+                    scalar1=b2_cols[:, t : t + 1],
+                    scalar2=0.0,
+                    op0=ALU.add,
+                    op1=ALU.max,
+                )
+            else:
+                nc.scalar.activation(
+                    out=tiles["h_by_t", q][:, t, :],
+                    in_=tiles["x1", q, t][:],
+                    func=ACT.Relu,
+                    bias=b2_cols[:, t : t + 1],
+                )
 
         def group_h(q):
             grouped = front.tile([P, QUAD * P * PACK], BF16, name="h_grouped", align_bytes=64)
@@ -320,6 +326,63 @@ def tile_edgefeaturenet_pb_t_kernel(
                 out=out_rows[:, PAIR * k : PAIR * (k + 1), :], in_=tiles["result", k][:]
             )
 
+        def means(q):
+            mean = stats.tile([P, QUAD], F32, name="mean")
+            nc.scalar.activation(
+                out=mean[:], in_=tiles["y_sum", q][:], func=ACT.Copy, scale=1.0 / E
+            )
+            tiles["mean", q] = mean
+
+        def scaled_columns(name, q, factors, source):
+            out_tile = stats.tile([P, QUAD], F32, name=name)
+            for c in range(QUAD):
+                nc.scalar.activation(
+                    out=out_tile[:, c : c + 1],
+                    in_=source[:, c : c + 1],
+                    func=ACT.Copy,
+                    scale=factors[:, c : c + 1],
+                )
+            tiles[name, q] = out_tile
+
+        def small_on_scalar(q):
+            scaled_columns("gain", q, mask[:, QUAD * q : QUAD * (q + 1)], tiles["rstd", q][:])
+            neg = stats.tile([P, QUAD], F32, name="neg_mean")
+            nc.scalar.activation(
+                out=neg[:], in_=tiles["y_sum", q][:], func=ACT.Copy, scale=-1.0 / E
+            )
+            scaled_columns("shift", q, neg[:], tiles["gain", q][:])
+
+        def centre_times_g(k, r, g_psum):
+            if r == 0:
+                tiles["normed", k] = rows.tile([P, PAIR, E], F32, name="normed")
+            c = PAIR * (k % 2) + r
+            nc.vector.scalar_tensor_tensor(
+                out=tiles["normed", k][:, r, :],
+                in0=tiles["y", k][:, r, :],
+                scalar=tiles["mean", k // 2][:, c : c + 1],
+                in1=g_psum[:],
+                op0=ALU.subtract,
+                op1=ALU.mult,
+            )
+
+        def times_gain(k, r):
+            if r == 0:
+                tiles["scaled", k] = rows.tile([P, PAIR, E], F32, name="scaled")
+            c = PAIR * (k % 2) + r
+            nc.scalar.activation(
+                out=tiles["scaled", k][:, r, :],
+                in_=tiles["normed", k][:, r, :],
+                func=ACT.Copy,
+                scale=tiles["gain", k // 2][:, c : c + 1],
+            )
+
+        def add_beta_and_store_each(k):
+            for r in range(PAIR):
+                add_beta(k, r)
+                nc.sync.dma_start(
+                    out=out_rows[:, PAIR * k + r, :], in_=tiles["result", k][:, r, :]
+                )
+
         def pair(stage, k, *more):
             if 0 <= k < PAIRS:
                 stage(k, *more)
@@ -329,23 +392,68 @@ def tile_edgefeaturenet_pb_t_kernel(
                 stage(q, *more)
 
         with tc.manual_schedule():
-            for k in range(-6, PAIRS + 5):
-                if k == -3:
-                    bank = psum_y.tile([P, E], F32, name="x2")
-                    repeat_on_all_partitions(0, bank)
-                    nc.vector.tensor_copy(out=b3_row[:], in_=bank[:])
-                    bank = psum_y.tile([P, E], F32, name="x2")
-                    repeat_on_all_partitions(1, bank)
+            w2_sorted = keep.tile([P, E], U32, name="w2_sorted", align_bytes=64)
+            nc.vector.tensor_copy(
+                out=w2_sorted[:].bitcast(I32).rearrange("p (t m) -> p t m", t=PACK),
+                in_=w2_words[:].bitcast(I32).rearrange("p (m t) -> p t m", t=PACK),
+            )
+            w2_sorted_plane = keep.tile([P, E], U8, name="w2_sorted_plane", align_bytes=64)
+            nc.vector.tensor_copy(
+                out=w2_sorted_plane[:].rearrange("p (t m) -> p m t", t=PACK),
+                in_=w2_plane[:].rearrange("p (m t) -> p m t", t=PACK),
+            )
+            b2_cols = keep.tile([P, PACK], F32, name="b2_cols")
+            nc.vector.tensor_copy(out=b2_cols[:], in_=b2_bf[:])
+            transpose_h1(0)
+            transpose_h1(1)
+            group_h1(0)
+            group_h1(1)
+            quantise_h1(0)
+            for t in range(PACK - 1):
+                layer1(0, t)
+            layer1(0, PACK - 1, spare_bank=True)
+            transpose_h1(2)
+            transpose_h1(3)
+            bias_relu(0, 0)
+            bias_relu(0, 1, on_vector=True)
+            bias_relu(0, 2)
+            bias_relu(0, 3, on_vector=True)
+            group_h1(2)
+            group_h1(3)
+            group_h(0)
+            transpose_h1(4)
+            transpose_h1(5)
+            quantise_h1(1)
+            repeat_on_all_partitions(0, beta_psum)
+            for t in range(PACK - 1):
+                layer1(1, t)
+            quantise_h(0)
+            nc.vector.tensor_copy(out=b3_row[:], in_=beta_psum[:])
+            layer2(0)
+            group_h1(4)
+            group_h1(5)
+            bias_relu(1, 0)
+            layer1(1, PACK - 1)
+            repeat_on_all_partitions(1, beta_psum)
+            transpose_h1(6)
+            transpose_h1(7)
+            bias_relu(1, 1)
+            bias_relu(1, 2)
+            bias_relu(1, 3)
+            mask = keep.tile([P, TILES], F32, name="mask")
+            nc.vector.tensor_copy(out=mask[:], in_=mask_bf[:])
+            for k in range(0, PAIRS - 2):
+                if k == 1:
                     for r in range(PAIR):
-                        nc.vector.tensor_copy(out=g_rows[:, r, :], in_=bank[:])
+                        nc.vector.tensor_copy(out=g_rows[:, r, :], in_=beta_psum[:])
                     repeat_on_all_partitions(2, beta_psum)
                 pair(add_b3, k)
                 pair(layer2, k + 1)
                 if k % 2 == 0:
-                    pair(group_h1, k + 4)
-                    pair(transpose_h1, k + 6)
-                    pair(group_h1, k + 5)
-                    pair(transpose_h1, k + 7)
+                    pair(group_h1, k + 6)
+                    pair(transpose_h1, k + 8)
+                    pair(group_h1, k + 7)
+                    pair(transpose_h1, k + 9)
                     pair(deviations, k)
                     pair(add_beta_first, k - 4)
                     pair(add_beta_second_and_store, k - 4)
@@ -372,3 +480,39 @@ def tile_edgefeaturenet_pb_t_kernel(
                     quad(bias_relu, (k + 3) // 2, 3)
                     pair(add_beta_first, k - 4)
                     pair(add_beta_second_and_store, k - 4)
+            last = PAIRS - 1
+            g_psum = psum_x.tile([P, E], F32, name="x1")
+            add_b3(last - 1)
+            layer2(last)
+            repeat_on_all_partitions(1, g_psum)
+            small_on_scalar(QUADS - 2)
+            add_b3(last)
+            normalise(last - 3, 0, False)
+            normalise(last - 3, 1, False)
+            scale_by_g(last - 3)
+            normalise(last - 2, 0, False)
+            normalise(last - 2, 1, False)
+            scale_by_g(last - 2)
+            deviations(last - 1)
+            deviations(last)
+            means(QUADS - 1)
+            reciprocal_std(QUADS - 1)
+            small_on_scalar(QUADS - 1)
+            add_beta_first(last - 5)
+            add_beta_second_and_store(last - 5)
+            add_beta_first(last - 4)
+            add_beta_second_and_store(last - 4)
+            add_beta_first(last - 3)
+            add_beta_second_and_store(last - 3)
+            centre_times_g(last, 0, g_psum)
+            centre_times_g(last, 1, g_psum)
+            normalise(last - 1, 0, False)
+            normalise(last - 1, 1, False)
+            scale_by_g(last - 1)
+            times_gain(last, 0)
+            times_gain(last, 1)
+            add_beta_first(last - 2)
+            add_beta_second_and_store(last - 2)
+            add_beta_first(last)
+            add_beta_second_and_store(last)
+            add_beta_and_store_each(last - 1)

@@ -20,6 +20,10 @@ PAIRS = TILES // PAIR
 QUAD = 4
 QUADS = TILES // QUAD
 EPS = 1e-5
+CORRECTED = 23
+VECTOR_TOKENS = 384
+EARLY_QUADS = 3
+LATE_QUADS = 13
 
 FLOPS = 2 * 2 * TOKENS * E * E
 
@@ -58,12 +62,12 @@ def tile_edgefeaturenet_pb_t_kernel(
     with tc.tile_pool(name="keep", bufs=1) as keep, tc.tile_pool(
         name="front", bufs=3
     ) as front, tc.tile_pool(name="rows", bufs=4) as rows, tc.tile_pool(
-        name="stats", bufs=3
-    ) as stats, tc.psum_pool(name="psum_t", bufs=2) as psum_t, tc.psum_pool(
-        name="psum_x", bufs=3
+        name="groups", bufs=3
+    ) as groups, tc.tile_pool(name="products", bufs=2) as products, tc.tile_pool(name="stats", bufs=3) as stats, tc.psum_pool(name="psum_t", bufs=2) as psum_t, tc.psum_pool(
+        name="psum_x", bufs=2
     ) as psum_x, tc.psum_pool(name="psum_y", bufs=2) as psum_y, tc.psum_pool(
-        name="psum_keep", bufs=1
-    ) as psum_keep:
+        name="psum_c", bufs=2
+    ) as psum_c:
         eps = keep.tile([P, 1], F32, name="eps")
         nc.vector.memset(eps[:], EPS)
         warm = keep.tile([P, 1], F32, name="warm")
@@ -100,12 +104,26 @@ def tile_edgefeaturenet_pb_t_kernel(
 
         ident_f32 = keep.tile([P, P], F32, name="ident_f32")
         make_identity(nc, ident_f32[:])
+        ident_bf = keep.tile([P, P], BF16, name="ident_bf")
+        make_identity(nc, ident_bf[:])
         ones = keep.tile([P, P], BF16, name="ones")
         nc.gpsimd.memset(ones[:], 1.0)
 
-        g_rows = keep.tile([P, PAIR, E], F32, name="g_rows")
+        g_row = keep.tile([P, 1, E], F32, name="g_row")
         b3_row = keep.tile([P, E], BF16, name="b3_row")
-        beta_psum = psum_keep.tile([P, E], F32, name="beta_psum")
+
+        columns = keep.tile([P, QUADS, P], BF16, name="columns")
+        nc.gpsimd.memset(columns[:].rearrange("p q c -> p (q c)").bitcast(I32), 0)
+        gains_rows = keep.tile([P, QUAD, E], BF16, name="gains_rows")
+        nc.gpsimd.memset(gains_rows[:].rearrange("p c n -> p (c n)").bitcast(I32), 0)
+        for c in range(QUAD):
+            nc.sync.dma_start(
+                out=gains_rows[c : 4 * QUAD : QUAD, c, :], in_=ln_g.partition_broadcast(4)
+            )
+            nc.sync.dma_start(
+                out=gains_rows[4 * QUAD + c : 4 * QUAD + c + 1, c, :],
+                in_=ln_b.rearrange("(o n) -> o n", o=1),
+            )
 
         def repeat_on_all_partitions(v, bank):
             nc.tensor.matmul(bank[:], lhsT=ones[:], rhs=vectors[:, v, :], start=True, stop=True)
@@ -178,13 +196,24 @@ def tile_edgefeaturenet_pb_t_kernel(
                     bias=b2_cols[:, t : t + 1],
                 )
 
-        def group_h(q):
-            grouped = front.tile([P, QUAD * P * PACK], BF16, name="h_grouped", align_bytes=64)
-            nc.vector.tensor_copy(
-                out=grouped[:].rearrange("p (c i t) -> p c t i", i=4, t=PACK),
-                in_=tiles["h_by_t", q][:].rearrange("p t (c i) -> p c t i", i=4),
+        def group_h(q, on_vector):
+            if not on_vector:
+                tiles["h_grouped", q] = front.tile(
+                    [P, QUAD * P * PACK], BF16, name="h_grouped", align_bytes=64
+                )
+            grouped = tiles["h_grouped", q]
+            split = VECTOR_TOKENS if EARLY_QUADS <= q < LATE_QUADS else QUAD * P
+            tokens = slice(0, split) if on_vector else slice(split, QUAD * P)
+            if tokens.start == tokens.stop:
+                return
+            target = grouped[:, PACK * tokens.start : PACK * tokens.stop].rearrange(
+                "p (c i t) -> p c t i", i=4, t=PACK
             )
-            tiles["h_grouped", q] = grouped
+            source = tiles["h_by_t", q][:, :, tokens].rearrange("p t (c i) -> p c t i", i=4)
+            if on_vector:
+                nc.vector.tensor_copy(out=target, in_=source)
+            else:
+                nc.scalar.copy(out=target, in_=source)
 
         def quantise_h(q):
             tiles["h_mx", q] = quantise_quad(nc, front, tiles["h_grouped", q], "h")
@@ -206,11 +235,42 @@ def tile_edgefeaturenet_pb_t_kernel(
                 )
                 tiles["x2", k, r] = product
 
+        def span(k):
+            first = PAIR * ((k + 1) % 2)
+            return slice(first, first + PAIR)
+
+        def y_pair(k):
+            j = (k + 1) // 2
+            if ("y", j) not in tiles:
+                tiles["y", j] = groups.tile([P, QUAD, E], F32, name="y")
+            return tiles["y", j][:, span(k), :]
+
+        def scale_group(j):
+            pairs = [k for k in (2 * j - 1, 2 * j) if 0 <= k < CORRECTED]
+            first, last_slot = span(pairs[0]).start, span(pairs[-1]).stop
+            scaled = products.tile([P, QUAD, E], F32, name="scaled_group")
+            nc.gpsimd.tensor_tensor(
+                out=scaled[:, first:last_slot, :],
+                in0=tiles["y", j][:, first:last_slot, :],
+                in1=g_row[:].to_broadcast([P, last_slot - first, E]),
+                op=ALU.mult,
+            )
+            for k in pairs:
+                tiles["scaled", k] = scaled[:, span(k), :]
+
+        def scale_on_vector(k, g_psum):
+            scaled = rows.tile([P, PAIR, E], F32, name="scaled")
+            for r in range(PAIR):
+                nc.vector.tensor_tensor(
+                    out=scaled[:, r, :], in0=y_pair(k)[:, r, :], in1=g_psum[:], op=ALU.mult
+                )
+            tiles["scaled", k] = scaled[:]
+
         def add_b3(k):
             q, half = k // 2, k % 2
             if half == 0:
                 tiles["y_sum", q] = stats.tile([P, QUAD], F32, name="y_sum")
-            y = rows.tile([P, PAIR, E], F32, name="y")
+            y = y_pair(k)
             for r in range(PAIR):
                 c = PAIR * half + r
                 nc.vector.scalar_tensor_tensor(
@@ -222,7 +282,6 @@ def tile_edgefeaturenet_pb_t_kernel(
                     op1=ALU.add,
                     accum_out=tiles["y_sum", q][:, c : c + 1],
                 )
-            tiles["y", k] = y
 
         def deviations(k):
             q, half = k // 2, k % 2
@@ -233,7 +292,7 @@ def tile_edgefeaturenet_pb_t_kernel(
                 dev_sq = front.tile([P, E], BF16, name="dev_sq")
                 nc.scalar.activation(
                     out=dev_sq[:],
-                    in_=tiles["y", k][:, r, :],
+                    in_=y_pair(k)[:, r, :],
                     func=ACT.Square,
                     scale=-1.0 * E,
                     bias=tiles["y_sum", q][:, c : c + 1],
@@ -282,7 +341,7 @@ def tile_edgefeaturenet_pb_t_kernel(
             if on_vector:
                 nc.vector.tensor_scalar(
                     out=tiles["normed", k][:, r, :],
-                    in0=tiles["y", k][:, r, :],
+                    in0=y_pair(k)[:, r, :],
                     scalar1=gain,
                     scalar2=shift,
                     op0=ALU.mult,
@@ -291,7 +350,7 @@ def tile_edgefeaturenet_pb_t_kernel(
             else:
                 nc.scalar.activation(
                     out=tiles["normed", k][:, r, :],
-                    in_=tiles["y", k][:, r, :],
+                    in_=y_pair(k)[:, r, :],
                     func=ACT.Identity,
                     scale=gain,
                     bias=shift,
@@ -300,9 +359,9 @@ def tile_edgefeaturenet_pb_t_kernel(
         def scale_by_g(k):
             scaled = rows.tile([P, PAIR, E], F32, name="scaled")
             nc.gpsimd.tensor_tensor(
-                out=scaled[:], in0=tiles["normed", k][:], in1=g_rows[:], op=ALU.mult
+                out=scaled[:], in0=tiles["normed", k][:], in1=g_row[:].to_broadcast([P, PAIR, E]), op=ALU.mult
             )
-            tiles["scaled", k] = scaled
+            tiles["scaled", k] = scaled[:]
 
         def add_beta(k, r):
             if r == 0:
@@ -310,7 +369,7 @@ def tile_edgefeaturenet_pb_t_kernel(
             i = PAIR * k + r
             nc.vector.scalar_tensor_tensor(
                 out=tiles["result", k][:, r, :],
-                in0=beta_psum[:],
+                in0=tiles["beta"][:],
                 scalar=mask[:, i : i + 1],
                 in1=tiles["scaled", k][:, r, :],
                 op0=ALU.mult,
@@ -322,6 +381,80 @@ def tile_edgefeaturenet_pb_t_kernel(
 
         def add_beta_second_and_store(k):
             add_beta(k, 1)
+            nc.sync.dma_start(
+                out=out_rows[:, PAIR * k : PAIR * (k + 1), :], in_=tiles["result", k][:]
+            )
+
+        def first_piece(q, on_gpsimd):
+            block = columns[:, q, :]
+            if on_gpsimd:
+                nc.gpsimd.tensor_copy(out=block[:, 0:QUAD], in_=tiles["shift", q][:])
+            else:
+                nc.scalar.copy(out=block[:, 0:QUAD], in_=tiles["shift", q][:])
+            rest = stats.tile([P, QUAD], F32, name="rest")
+            for c in range(QUAD):
+                nc.scalar.activation(
+                    out=rest[:, c : c + 1],
+                    in_=block[:, c : c + 1],
+                    func=ACT.Identity,
+                    scale=-1.0,
+                    bias=tiles["shift", q][:, c : c + 1],
+                )
+            tiles["rest", q] = rest
+
+        def second_piece(q):
+            nc.scalar.copy(out=columns[:, q, QUAD : 2 * QUAD], in_=tiles["rest", q][:])
+
+        def third_piece(q):
+            block = columns[:, q, :]
+            for c in range(QUAD):
+                nc.scalar.activation(
+                    out=block[:, 2 * QUAD + c : 2 * QUAD + c + 1],
+                    in_=block[:, QUAD + c : QUAD + c + 1],
+                    func=ACT.Identity,
+                    scale=-1.0,
+                    bias=tiles["rest", q][:, c : c + 1],
+                )
+            turned = psum_t.tile([P, P], BF16, name="h1T")
+            nc.tensor.transpose(turned[:], columns[:, q, :], ident_bf[:])
+            tiles["turned", q] = turned
+
+        def coefficients(q):
+            rows_of_tokens = stats.tile([P, P], BF16, name="coefficients")
+            nc.scalar.copy(out=rows_of_tokens[:], in_=tiles["turned", q][:])
+            tiles["coefficients", q] = rows_of_tokens
+
+        def correction(k, r):
+            bank = psum_c.tile([P, E], F32, name="correction")
+            nc.tensor.matmul(
+                bank[:],
+                lhsT=tiles["coefficients", k // 2][:],
+                rhs=gains_rows[:, PAIR * (k % 2) + r, :],
+                start=True,
+                stop=True,
+            )
+            tiles["correction", k, r] = bank
+
+        def add_correction(k, r):
+            if r == 0:
+                tiles["result", k] = rows.tile([P, PAIR, E], F32, name="result")
+            c = PAIR * (k % 2) + r
+            nc.vector.scalar_tensor_tensor(
+                out=tiles["result", k][:, r, :],
+                in0=tiles["scaled", k][:, r, :],
+                scalar=tiles["gain", k // 2][:, c : c + 1],
+                in1=tiles["correction", k, r][:],
+                op0=ALU.mult,
+                op1=ALU.add,
+            )
+
+        def finish(k):
+            if k < CORRECTED:
+                add_correction(k, 0)
+                add_correction(k, 1)
+            else:
+                add_beta(k, 0)
+                add_beta(k, 1)
             nc.sync.dma_start(
                 out=out_rows[:, PAIR * k : PAIR * (k + 1), :], in_=tiles["result", k][:]
             )
@@ -358,7 +491,7 @@ def tile_edgefeaturenet_pb_t_kernel(
             c = PAIR * (k % 2) + r
             nc.vector.scalar_tensor_tensor(
                 out=tiles["normed", k][:, r, :],
-                in0=tiles["y", k][:, r, :],
+                in0=y_pair(k)[:, r, :],
                 scalar=tiles["mean", k // 2][:, c : c + 1],
                 in1=g_psum[:],
                 op0=ALU.subtract,
@@ -367,7 +500,7 @@ def tile_edgefeaturenet_pb_t_kernel(
 
         def times_gain(k, r):
             if r == 0:
-                tiles["scaled", k] = rows.tile([P, PAIR, E], F32, name="scaled")
+                tiles["scaled", k] = rows.tile([P, PAIR, E], F32, name="scaled")[:]
             c = PAIR * (k % 2) + r
             nc.scalar.activation(
                 out=tiles["scaled", k][:, r, :],
@@ -409,9 +542,10 @@ def tile_edgefeaturenet_pb_t_kernel(
             group_h1(0)
             group_h1(1)
             quantise_h1(0)
-            for t in range(PACK - 1):
-                layer1(0, t)
-            layer1(0, PACK - 1, spare_bank=True)
+            layer1(0, 0)
+            layer1(0, 1)
+            layer1(0, 2, spare_bank=True)
+            layer1(0, 3, spare_bank=True)
             transpose_h1(2)
             transpose_h1(3)
             bias_relu(0, 0)
@@ -420,68 +554,101 @@ def tile_edgefeaturenet_pb_t_kernel(
             bias_relu(0, 3, on_vector=True)
             group_h1(2)
             group_h1(3)
-            group_h(0)
+            group_h(0, False)
+            group_h(0, True)
             transpose_h1(4)
             transpose_h1(5)
             quantise_h1(1)
-            repeat_on_all_partitions(0, beta_psum)
-            for t in range(PACK - 1):
-                layer1(1, t)
+            bank = psum_c.tile([P, E], F32, name="correction")
+            repeat_on_all_partitions(0, bank)
+            layer1(1, 0)
+            layer1(1, 1)
             quantise_h(0)
-            nc.vector.tensor_copy(out=b3_row[:], in_=beta_psum[:])
+            nc.vector.tensor_copy(out=b3_row[:], in_=bank[:])
             layer2(0)
             group_h1(4)
             group_h1(5)
             bias_relu(1, 0)
-            layer1(1, PACK - 1)
-            repeat_on_all_partitions(1, beta_psum)
+            bias_relu(1, 1, on_vector=True)
+            layer1(1, 2)
+            layer1(1, 3)
+            bank = psum_c.tile([P, E], F32, name="correction")
+            repeat_on_all_partitions(1, bank)
             transpose_h1(6)
             transpose_h1(7)
-            bias_relu(1, 1)
             bias_relu(1, 2)
-            bias_relu(1, 3)
+            add_b3(0)
+            bias_relu(1, 3, on_vector=True)
+            nc.vector.tensor_copy(out=g_row[:, 0, :], in_=bank[:])
+            group_h(1, False)
             mask = keep.tile([P, TILES], F32, name="mask")
             nc.vector.tensor_copy(out=mask[:], in_=mask_bf[:])
+            nc.vector.tensor_copy(
+                out=columns[:, :, 4 * QUAD : 5 * QUAD],
+                in_=mask_bf[:].rearrange("p (q c) -> p q c", c=QUAD),
+            )
             for k in range(0, PAIRS - 2):
-                if k == 1:
-                    for r in range(PAIR):
-                        nc.vector.tensor_copy(out=g_rows[:, r, :], in_=beta_psum[:])
-                    repeat_on_all_partitions(2, beta_psum)
-                pair(add_b3, k)
-                pair(layer2, k + 1)
+                if k == CORRECTED + 4:
+                    tiles["beta"] = psum_c.tile([P, E], F32, name="correction")
+                    repeat_on_all_partitions(2, tiles["beta"])
+                if k > 0:
+                    add_b3(k)
+                pair(finish, k - 4)
                 if k % 2 == 0:
+                    q = k // 2
+                    pair(layer2, k + 1)
                     pair(group_h1, k + 6)
-                    pair(transpose_h1, k + 8)
                     pair(group_h1, k + 7)
-                    pair(transpose_h1, k + 9)
                     pair(deviations, k)
-                    pair(add_beta_first, k - 4)
-                    pair(add_beta_second_and_store, k - 4)
-                    quad(gains, (k - 2) // 2)
-                    quad(group_h, (k + 2) // 2)
-                    quad(shifts, (k - 2) // 2)
-                    quad(quantise_h1, (k + 4) // 2)
-                    for t in range(PACK - 1):
-                        quad(layer1, (k + 4) // 2, t)
-                    pair(normalise, k - 2, 0, True)
-                    pair(normalise, k - 2, 1, False)
-                    pair(normalise, k - 1, 0, False)
-                    pair(normalise, k - 1, 1, False)
-                    quad(quantise_h, (k + 2) // 2)
-                    pair(scale_by_g, k - 2)
-                    pair(scale_by_g, k - 1)
+                    quad(gains, q - 1)
+                    quad(quantise_h1, q + 2)
+                    quad(shifts, q - 1)
+                    quad(group_h, q + 1, True)
+                    quad(quantise_h, q + 1)
+                    quad(layer1, q + 2, 0)
+                    quad(layer1, q + 2, 1)
+                    if 0 <= k - 2 < CORRECTED:
+                        first_piece(q - 1, True)
+                    for i in (k - 2, k - 1):
+                        if i >= CORRECTED:
+                            for r in range(PAIR):
+                                normalise(i, r, False)
+                    if k == 0:
+                        scale_on_vector(0, bank)
+                    elif k - 1 < CORRECTED:
+                        scale_group(q)
+                    for i in (k - 2, k - 1):
+                        if i >= CORRECTED:
+                            scale_by_g(i)
+                    if 0 <= k - 3 < CORRECTED:
+                        correction(k - 3, 0)
+                        correction(k - 3, 1)
                 else:
-                    quad(bias_relu, (k + 3) // 2, 0)
-                    quad(layer1, (k + 3) // 2, PACK - 1)
-                    quad(bias_relu, (k + 3) // 2, 1)
+                    q = (k + 3) // 2
+                    p = (k - 3) // 2
+                    quad(bias_relu, q, 0)
+                    quad(layer1, q, 2)
+                    if 0 <= 2 * p < CORRECTED:
+                        second_piece(p)
+                    quad(bias_relu, q, 1)
+                    pair(layer2, k + 1)
+                    quad(layer1, q, 3)
+                    if 0 <= 2 * p < CORRECTED:
+                        third_piece(p)
                     pair(deviations, k)
+                    if 0 <= 2 * p < CORRECTED:
+                        coefficients(p)
                     quad(reciprocal_std, (k - 1) // 2)
-                    quad(bias_relu, (k + 3) // 2, 2)
-                    quad(bias_relu, (k + 3) // 2, 3)
-                    pair(add_beta_first, k - 4)
-                    pair(add_beta_second_and_store, k - 4)
+                    quad(bias_relu, q, 2)
+                    quad(bias_relu, q, 3)
+                    quad(group_h, q, False)
+                    if 0 <= k - 3 < CORRECTED:
+                        correction(k - 3, 0)
+                        correction(k - 3, 1)
+                    pair(transpose_h1, k + 7)
+                    pair(transpose_h1, k + 8)
             last = PAIRS - 1
-            g_psum = psum_x.tile([P, E], F32, name="x1")
+            g_psum = psum_c.tile([P, E], F32, name="correction")
             add_b3(last - 1)
             layer2(last)
             repeat_on_all_partitions(1, g_psum)

@@ -21,7 +21,7 @@ QUAD = 4
 QUADS = TILES // QUAD
 EPS = 1e-5
 CORRECTED = 23
-VECTOR_TOKENS = 384
+VECTOR_TOKENS = 416
 EARLY_QUADS = 3
 LATE_QUADS = 13
 
@@ -62,6 +62,8 @@ def tile_edgefeaturenet_pb_t_kernel(
     with tc.tile_pool(name="keep", bufs=1) as keep, tc.tile_pool(
         name="front", bufs=3
     ) as front, tc.tile_pool(name="rows", bufs=4) as rows, tc.tile_pool(
+        name="late", bufs=4
+    ) as late, tc.tile_pool(
         name="groups", bufs=3
     ) as groups, tc.tile_pool(name="products", bufs=2) as products, tc.tile_pool(name="stats", bufs=3) as stats, tc.psum_pool(name="psum_t", bufs=2) as psum_t, tc.psum_pool(
         name="psum_x", bufs=2
@@ -109,7 +111,7 @@ def tile_edgefeaturenet_pb_t_kernel(
         ones = keep.tile([P, P], BF16, name="ones")
         nc.gpsimd.memset(ones[:], 1.0)
 
-        g_row = keep.tile([P, 1, E], F32, name="g_row")
+        g_rows = keep.tile([P, QUAD, E], F32, name="g_rows")
         b3_row = keep.tile([P, E], BF16, name="b3_row")
 
         columns = keep.tile([P, QUADS, P], BF16, name="columns")
@@ -245,21 +247,26 @@ def tile_edgefeaturenet_pb_t_kernel(
                 tiles["y", j] = groups.tile([P, QUAD, E], F32, name="y")
             return tiles["y", j][:, span(k), :]
 
+        def hold_group(j):
+            scaled = products.tile([P, QUAD, E], F32, name="scaled_group")
+            nc.vector.memset(scaled[:, span(2 * j - 1).start, 0:1], 0.0)
+            tiles["scaled_group", j] = scaled
+
         def scale_group(j):
             pairs = [k for k in (2 * j - 1, 2 * j) if 0 <= k < CORRECTED]
             first, last_slot = span(pairs[0]).start, span(pairs[-1]).stop
-            scaled = products.tile([P, QUAD, E], F32, name="scaled_group")
+            scaled = tiles["scaled_group", j]
             nc.gpsimd.tensor_tensor(
                 out=scaled[:, first:last_slot, :],
                 in0=tiles["y", j][:, first:last_slot, :],
-                in1=g_row[:].to_broadcast([P, last_slot - first, E]),
+                in1=g_rows[:, first:last_slot, :],
                 op=ALU.mult,
             )
             for k in pairs:
                 tiles["scaled", k] = scaled[:, span(k), :]
 
         def scale_on_vector(k, g_psum):
-            scaled = rows.tile([P, PAIR, E], F32, name="scaled")
+            scaled = late.tile([P, PAIR, E], F32, name="scaled")
             for r in range(PAIR):
                 nc.vector.tensor_tensor(
                     out=scaled[:, r, :], in0=y_pair(k)[:, r, :], in1=g_psum[:], op=ALU.mult
@@ -283,11 +290,11 @@ def tile_edgefeaturenet_pb_t_kernel(
                     accum_out=tiles["y_sum", q][:, c : c + 1],
                 )
 
-        def deviations(k):
+        def deviations(k, tiles_of_pair=range(PAIR)):
             q, half = k // 2, k % 2
-            if half == 0:
+            if half == 0 and 0 in tiles_of_pair:
                 tiles["dev_sq_sum", q] = stats.tile([P, QUAD], F32, name="dev_sq_sum")
-            for r in range(PAIR):
+            for r in tiles_of_pair:
                 c = PAIR * half + r
                 dev_sq = front.tile([P, E], BF16, name="dev_sq")
                 nc.scalar.activation(
@@ -334,7 +341,7 @@ def tile_edgefeaturenet_pb_t_kernel(
 
         def normalise(k, r, on_vector):
             if r == 0:
-                tiles["normed", k] = rows.tile([P, PAIR, E], F32, name="normed")
+                tiles["normed", k] = late.tile([P, PAIR, E], F32, name="normed")
             c = PAIR * (k % 2) + r
             gain = tiles["gain", k // 2][:, c : c + 1]
             shift = tiles["shift", k // 2][:, c : c + 1]
@@ -357,9 +364,9 @@ def tile_edgefeaturenet_pb_t_kernel(
                 )
 
         def scale_by_g(k):
-            scaled = rows.tile([P, PAIR, E], F32, name="scaled")
+            scaled = late.tile([P, PAIR, E], F32, name="scaled")
             nc.gpsimd.tensor_tensor(
-                out=scaled[:], in0=tiles["normed", k][:], in1=g_row[:].to_broadcast([P, PAIR, E]), op=ALU.mult
+                out=scaled[:], in0=tiles["normed", k][:], in1=g_rows[:, 0:PAIR, :], op=ALU.mult
             )
             tiles["scaled", k] = scaled[:]
 
@@ -385,17 +392,15 @@ def tile_edgefeaturenet_pb_t_kernel(
                 out=out_rows[:, PAIR * k : PAIR * (k + 1), :], in_=tiles["result", k][:]
             )
 
-        def first_piece(q, on_gpsimd):
-            block = columns[:, q, :]
-            if on_gpsimd:
-                nc.gpsimd.tensor_copy(out=block[:, 0:QUAD], in_=tiles["shift", q][:])
-            else:
-                nc.scalar.copy(out=block[:, 0:QUAD], in_=tiles["shift", q][:])
+        def first_piece(q):
+            nc.scalar.copy(out=columns[:, q, 0:QUAD], in_=tiles["shift", q][:])
+
+        def first_rest(q):
             rest = stats.tile([P, QUAD], F32, name="rest")
             for c in range(QUAD):
                 nc.scalar.activation(
                     out=rest[:, c : c + 1],
-                    in_=block[:, c : c + 1],
+                    in_=columns[:, q, c : c + 1],
                     func=ACT.Identity,
                     scale=-1.0,
                     bias=tiles["shift", q][:, c : c + 1],
@@ -487,7 +492,7 @@ def tile_edgefeaturenet_pb_t_kernel(
 
         def centre_times_g(k, r, g_psum):
             if r == 0:
-                tiles["normed", k] = rows.tile([P, PAIR, E], F32, name="normed")
+                tiles["normed", k] = late.tile([P, PAIR, E], F32, name="normed")
             c = PAIR * (k % 2) + r
             nc.vector.scalar_tensor_tensor(
                 out=tiles["normed", k][:, r, :],
@@ -500,7 +505,7 @@ def tile_edgefeaturenet_pb_t_kernel(
 
         def times_gain(k, r):
             if r == 0:
-                tiles["scaled", k] = rows.tile([P, PAIR, E], F32, name="scaled")[:]
+                tiles["scaled", k] = late.tile([P, PAIR, E], F32, name="scaled")[:]
             c = PAIR * (k % 2) + r
             nc.scalar.activation(
                 out=tiles["scaled", k][:, r, :],
@@ -579,7 +584,6 @@ def tile_edgefeaturenet_pb_t_kernel(
             bias_relu(1, 2)
             add_b3(0)
             bias_relu(1, 3, on_vector=True)
-            nc.vector.tensor_copy(out=g_row[:, 0, :], in_=bank[:])
             group_h(1, False)
             mask = keep.tile([P, TILES], F32, name="mask")
             nc.vector.tensor_copy(out=mask[:], in_=mask_bf[:])
@@ -599,16 +603,21 @@ def tile_edgefeaturenet_pb_t_kernel(
                     pair(layer2, k + 1)
                     pair(group_h1, k + 6)
                     pair(group_h1, k + 7)
-                    pair(deviations, k)
+                    pair(deviations, k, (0,))
                     quad(gains, q - 1)
-                    quad(quantise_h1, q + 2)
-                    quad(shifts, q - 1)
                     quad(group_h, q + 1, True)
+                    quad(shifts, q - 1)
+                    quad(quantise_h1, q + 2)
+                    if k > 0 and k - 1 < CORRECTED:
+                        hold_group(q)
                     quad(quantise_h, q + 1)
                     quad(layer1, q + 2, 0)
                     quad(layer1, q + 2, 1)
                     if 0 <= k - 2 < CORRECTED:
-                        first_piece(q - 1, True)
+                        first_piece(q - 1)
+                    pair(deviations, k, (1,))
+                    if 0 <= k - 2 < CORRECTED:
+                        first_rest(q - 1)
                     for i in (k - 2, k - 1):
                         if i >= CORRECTED:
                             for r in range(PAIR):
@@ -635,6 +644,10 @@ def tile_edgefeaturenet_pb_t_kernel(
                     quad(layer1, q, 3)
                     if 0 <= 2 * p < CORRECTED:
                         third_piece(p)
+                    if k == 1:
+                        for r in range(PAIR):
+                            nc.scalar.copy(out=g_rows[:, r, :], in_=bank[:])
+                            nc.vector.tensor_copy(out=g_rows[:, PAIR + r, :], in_=bank[:])
                     pair(deviations, k)
                     if 0 <= 2 * p < CORRECTED:
                         coefficients(p)

@@ -21,8 +21,9 @@ QUAD = 4
 QUADS = TILES // QUAD
 EPS = 1e-5
 CORRECTED = 23
-VECTOR_TOKENS = 416
+VECTOR_TOKENS = 384
 EARLY_QUADS = 3
+HALF = 256
 LATE_QUADS = 13
 
 FLOPS = 2 * 2 * TOKENS * E * E
@@ -198,27 +199,37 @@ def tile_edgefeaturenet_pb_t_kernel(
                     bias=b2_cols[:, t : t + 1],
                 )
 
-        def group_h(q, on_vector):
-            if not on_vector:
+        def group_h(q, part):
+            if ("h_grouped", q) not in tiles:
                 tiles["h_grouped", q] = front.tile(
                     [P, QUAD * P * PACK], BF16, name="h_grouped", align_bytes=64
                 )
-            grouped = tiles["h_grouped", q]
             split = VECTOR_TOKENS if EARLY_QUADS <= q < LATE_QUADS else QUAD * P
-            tokens = slice(0, split) if on_vector else slice(split, QUAD * P)
-            if tokens.start == tokens.stop:
+            first, stop = ((0, HALF), (HALF, split), (split, QUAD * P))[part]
+            if first == stop:
                 return
-            target = grouped[:, PACK * tokens.start : PACK * tokens.stop].rearrange(
+            target = tiles["h_grouped", q][:, PACK * first : PACK * stop].rearrange(
                 "p (c i t) -> p c t i", i=4, t=PACK
             )
-            source = tiles["h_by_t", q][:, :, tokens].rearrange("p t (c i) -> p c t i", i=4)
-            if on_vector:
-                nc.vector.tensor_copy(out=target, in_=source)
-            else:
+            source = tiles["h_by_t", q][:, :, first:stop].rearrange("p t (c i) -> p c t i", i=4)
+            if part == 2:
                 nc.scalar.copy(out=target, in_=source)
+            else:
+                nc.vector.tensor_copy(out=target, in_=source)
 
-        def quantise_h(q):
-            tiles["h_mx", q] = quantise_quad(nc, front, tiles["h_grouped", q], "h")
+        def quantise_h(q, half):
+            if half == 0:
+                tiles["h_mx", q] = (
+                    front.tile([P, QUAD * P], U32, name="h_codes", align_bytes=64),
+                    front.tile([P, QUAD * P], U8, name="h_scales", align_bytes=64),
+                )
+            codes, scales = tiles["h_mx", q]
+            cols = slice(half * HALF, (half + 1) * HALF)
+            nc.vector.quantize_mx(
+                out=codes[:, cols].bitcast(FP8X4),
+                scales=scales[:, cols],
+                in_=tiles["h_grouped", q][:, PACK * cols.start : PACK * cols.stop],
+            )
 
         def layer2(k):
             codes, scales = tiles["h_mx", k // 2]
@@ -249,7 +260,7 @@ def tile_edgefeaturenet_pb_t_kernel(
 
         def hold_group(j):
             scaled = products.tile([P, QUAD, E], F32, name="scaled_group")
-            nc.vector.memset(scaled[:, span(2 * j - 1).start, 0:1], 0.0)
+            nc.vector.memset(scaled[:, span(max(2 * j - 1, 0)).start, 0:1], 0.0)
             tiles["scaled_group", j] = scaled
 
         def scale_group(j):
@@ -559,8 +570,8 @@ def tile_edgefeaturenet_pb_t_kernel(
             bias_relu(0, 3, on_vector=True)
             group_h1(2)
             group_h1(3)
-            group_h(0, False)
-            group_h(0, True)
+            group_h(0, 0)
+            group_h(0, 1)
             transpose_h1(4)
             transpose_h1(5)
             quantise_h1(1)
@@ -568,8 +579,9 @@ def tile_edgefeaturenet_pb_t_kernel(
             repeat_on_all_partitions(0, bank)
             layer1(1, 0)
             layer1(1, 1)
-            quantise_h(0)
-            nc.vector.tensor_copy(out=b3_row[:], in_=bank[:])
+            quantise_h(0, 0)
+            quantise_h(0, 1)
+            nc.scalar.copy(out=b3_row[:], in_=bank[:])
             layer2(0)
             group_h1(4)
             group_h1(5)
@@ -584,7 +596,17 @@ def tile_edgefeaturenet_pb_t_kernel(
             bias_relu(1, 2)
             add_b3(0)
             bias_relu(1, 3, on_vector=True)
-            group_h(1, False)
+            for r in range(PAIR):
+                nc.scalar.copy(out=g_rows[:, PAIR + r, :], in_=bank[:])
+            nc.gpsimd.tensor_scalar(
+                out=g_rows[:, 0:PAIR, :],
+                in0=g_rows[:, PAIR:QUAD, :],
+                scalar1=1.0,
+                scalar2=0.0,
+                op0=ALU.mult,
+                op1=ALU.add,
+            )
+            group_h(1, 2)
             mask = keep.tile([P, TILES], F32, name="mask")
             nc.vector.tensor_copy(out=mask[:], in_=mask_bf[:])
             nc.vector.tensor_copy(
@@ -605,12 +627,14 @@ def tile_edgefeaturenet_pb_t_kernel(
                     pair(group_h1, k + 7)
                     pair(deviations, k, (0,))
                     quad(gains, q - 1)
-                    quad(group_h, q + 1, True)
-                    quad(shifts, q - 1)
                     quad(quantise_h1, q + 2)
-                    if k > 0 and k - 1 < CORRECTED:
+                    quad(shifts, q - 1)
+                    quad(group_h, q + 1, 0)
+                    quad(group_h, q + 1, 1)
+                    quad(quantise_h, q + 1, 0)
+                    if k - 1 < CORRECTED:
                         hold_group(q)
-                    quad(quantise_h, q + 1)
+                    quad(quantise_h, q + 1, 1)
                     quad(layer1, q + 2, 0)
                     quad(layer1, q + 2, 1)
                     if 0 <= k - 2 < CORRECTED:
@@ -622,9 +646,7 @@ def tile_edgefeaturenet_pb_t_kernel(
                         if i >= CORRECTED:
                             for r in range(PAIR):
                                 normalise(i, r, False)
-                    if k == 0:
-                        scale_on_vector(0, bank)
-                    elif k - 1 < CORRECTED:
+                    if k - 1 < CORRECTED:
                         scale_group(q)
                     for i in (k - 2, k - 1):
                         if i >= CORRECTED:
@@ -644,17 +666,13 @@ def tile_edgefeaturenet_pb_t_kernel(
                     quad(layer1, q, 3)
                     if 0 <= 2 * p < CORRECTED:
                         third_piece(p)
-                    if k == 1:
-                        for r in range(PAIR):
-                            nc.scalar.copy(out=g_rows[:, r, :], in_=bank[:])
-                            nc.vector.tensor_copy(out=g_rows[:, PAIR + r, :], in_=bank[:])
                     pair(deviations, k)
                     if 0 <= 2 * p < CORRECTED:
                         coefficients(p)
                     quad(reciprocal_std, (k - 1) // 2)
                     quad(bias_relu, q, 2)
                     quad(bias_relu, q, 3)
-                    quad(group_h, q, False)
+                    quad(group_h, q, 2)
                     if 0 <= k - 3 < CORRECTED:
                         correction(k - 3, 0)
                         correction(k - 3, 1)

@@ -21,10 +21,11 @@ QUAD = 4
 QUADS = TILES // QUAD
 EPS = 1e-5
 CORRECTED = 23
-VECTOR_TOKENS = 384
+VECTOR_TOKENS = 352
 EARLY_QUADS = 3
 HALF = 256
 LATE_QUADS = 13
+LATE_TOKENS = 448
 
 FLOPS = 2 * 2 * TOKENS * E * E
 
@@ -109,6 +110,8 @@ def tile_edgefeaturenet_pb_t_kernel(
         make_identity(nc, ident_f32[:])
         ident_bf = keep.tile([P, P], BF16, name="ident_bf")
         make_identity(nc, ident_bf[:])
+        minus_ident = keep.tile([P, P], BF16, name="minus_ident")
+        nc.scalar.mul(minus_ident[:], ident_bf[:], -1.0)
         ones = keep.tile([P, P], BF16, name="ones")
         nc.gpsimd.memset(ones[:], 1.0)
 
@@ -116,9 +119,9 @@ def tile_edgefeaturenet_pb_t_kernel(
         b3_row = keep.tile([P, E], BF16, name="b3_row")
 
         columns = keep.tile([P, QUADS, P], BF16, name="columns")
-        nc.gpsimd.memset(columns[:].rearrange("p q c -> p (q c)").bitcast(I32), 0)
+        nc.vector.memset(columns[:].rearrange("p q c -> p (q c)").bitcast(I32), 0)
         gains_rows = keep.tile([P, QUAD, E], BF16, name="gains_rows")
-        nc.gpsimd.memset(gains_rows[:].rearrange("p c n -> p (c n)").bitcast(I32), 0)
+        nc.vector.memset(gains_rows[:].rearrange("p c n -> p (c n)").bitcast(I32), 0)
         for c in range(QUAD):
             nc.sync.dma_start(
                 out=gains_rows[c : 4 * QUAD : QUAD, c, :], in_=ln_g.partition_broadcast(4)
@@ -204,7 +207,7 @@ def tile_edgefeaturenet_pb_t_kernel(
                 tiles["h_grouped", q] = front.tile(
                     [P, QUAD * P * PACK], BF16, name="h_grouped", align_bytes=64
                 )
-            split = VECTOR_TOKENS if EARLY_QUADS <= q < LATE_QUADS else QUAD * P
+            split = QUAD * P if q < EARLY_QUADS else VECTOR_TOKENS if q < LATE_QUADS else LATE_TOKENS
             first, stop = ((0, HALF), (HALF, split), (split, QUAD * P))[part]
             if first == stop:
                 return
@@ -231,9 +234,9 @@ def tile_edgefeaturenet_pb_t_kernel(
                 in_=tiles["h_grouped", q][:, PACK * cols.start : PACK * cols.stop],
             )
 
-        def layer2(k):
+        def layer2(k, tiles_of_pair=range(PAIR)):
             codes, scales = tiles["h_mx", k // 2]
-            for r in range(PAIR):
+            for r in tiles_of_pair:
                 first = (PAIR * (k % 2) + r) * P
                 token_cols = slice(first, first + P)
                 product = psum_y.tile([P, E], F32, name="x2")
@@ -258,15 +261,16 @@ def tile_edgefeaturenet_pb_t_kernel(
                 tiles["y", j] = groups.tile([P, QUAD, E], F32, name="y")
             return tiles["y", j][:, span(k), :]
 
-        def hold_group(j):
-            scaled = products.tile([P, QUAD, E], F32, name="scaled_group")
-            nc.vector.memset(scaled[:, span(max(2 * j - 1, 0)).start, 0:1], 0.0)
-            tiles["scaled_group", j] = scaled
+        def hold_pair(k):
+            tiles["scaled", k] = late.tile([P, PAIR, E], F32, name="scaled")[:]
+            nc.vector.memset(tiles["scaled", k][:, 0, 0:1], 0.0)
 
         def scale_group(j):
             pairs = [k for k in (2 * j - 1, 2 * j) if 0 <= k < CORRECTED]
             first, last_slot = span(pairs[0]).start, span(pairs[-1]).stop
-            scaled = tiles["scaled_group", j]
+            scaled = products.tile([P, QUAD, E], F32, name="scaled_group")
+            if j == 0:
+                nc.vector.memset(scaled[:, span(0).start, 0:1], 0.0)
             nc.gpsimd.tensor_tensor(
                 out=scaled[:, first:last_slot, :],
                 in0=tiles["y", j][:, first:last_slot, :],
@@ -375,11 +379,14 @@ def tile_edgefeaturenet_pb_t_kernel(
                 )
 
         def scale_by_g(k):
-            scaled = late.tile([P, PAIR, E], F32, name="scaled")
+            if ("scaled", k) not in tiles:
+                tiles["scaled", k] = late.tile([P, PAIR, E], F32, name="scaled")[:]
             nc.gpsimd.tensor_tensor(
-                out=scaled[:], in0=tiles["normed", k][:], in1=g_rows[:, 0:PAIR, :], op=ALU.mult
+                out=tiles["scaled", k],
+                in0=tiles["normed", k][:],
+                in1=g_rows[:, 0:PAIR, :],
+                op=ALU.mult,
             )
-            tiles["scaled", k] = scaled[:]
 
         def add_beta(k, r):
             if r == 0:
@@ -404,33 +411,29 @@ def tile_edgefeaturenet_pb_t_kernel(
             )
 
         def first_piece(q):
-            nc.scalar.copy(out=columns[:, q, 0:QUAD], in_=tiles["shift", q][:])
+            nc.gpsimd.tensor_copy(out=columns[:, q, 0:QUAD], in_=tiles["shift", q][:])
 
-        def first_rest(q):
-            rest = stats.tile([P, QUAD], F32, name="rest")
-            for c in range(QUAD):
-                nc.scalar.activation(
-                    out=rest[:, c : c + 1],
-                    in_=columns[:, q, c : c + 1],
-                    func=ACT.Identity,
-                    scale=-1.0,
-                    bias=tiles["shift", q][:, c : c + 1],
+        def what_is_left(q, pieces):
+            left = psum_t.tile([P, QUAD], F32, name="h1T")
+            nc.tensor.matmul(
+                left[:], lhsT=ident_f32[:], rhs=tiles["shift", q][:], start=True, stop=False
+            )
+            for j in range(pieces):
+                nc.tensor.matmul(
+                    left[:],
+                    lhsT=minus_ident[:],
+                    rhs=columns[:, q, j * QUAD : (j + 1) * QUAD],
+                    start=False,
+                    stop=j == pieces - 1,
                 )
-            tiles["rest", q] = rest
+            tiles["left", q] = left
 
-        def second_piece(q):
-            nc.scalar.copy(out=columns[:, q, QUAD : 2 * QUAD], in_=tiles["rest", q][:])
+        def next_piece(q, j):
+            nc.scalar.copy(
+                out=columns[:, q, j * QUAD : (j + 1) * QUAD], in_=tiles["left", q][:]
+            )
 
-        def third_piece(q):
-            block = columns[:, q, :]
-            for c in range(QUAD):
-                nc.scalar.activation(
-                    out=block[:, 2 * QUAD + c : 2 * QUAD + c + 1],
-                    in_=block[:, QUAD + c : QUAD + c + 1],
-                    func=ACT.Identity,
-                    scale=-1.0,
-                    bias=tiles["rest", q][:, c : c + 1],
-                )
+        def turn(q):
             turned = psum_t.tile([P, P], BF16, name="h1T")
             nc.tensor.transpose(turned[:], columns[:, q, :], ident_bf[:])
             tiles["turned", q] = turned
@@ -475,16 +478,9 @@ def tile_edgefeaturenet_pb_t_kernel(
                 out=out_rows[:, PAIR * k : PAIR * (k + 1), :], in_=tiles["result", k][:]
             )
 
-        def means(q):
-            mean = stats.tile([P, QUAD], F32, name="mean")
-            nc.scalar.activation(
-                out=mean[:], in_=tiles["y_sum", q][:], func=ACT.Copy, scale=1.0 / E
-            )
-            tiles["mean", q] = mean
-
-        def scaled_columns(name, q, factors, source):
+        def scaled_columns(name, q, factors, source, count=QUAD):
             out_tile = stats.tile([P, QUAD], F32, name=name)
-            for c in range(QUAD):
+            for c in range(count):
                 nc.scalar.activation(
                     out=out_tile[:, c : c + 1],
                     in_=source[:, c : c + 1],
@@ -493,13 +489,18 @@ def tile_edgefeaturenet_pb_t_kernel(
                 )
             tiles[name, q] = out_tile
 
-        def small_on_scalar(q):
-            scaled_columns("gain", q, mask[:, QUAD * q : QUAD * (q + 1)], tiles["rstd", q][:])
+        def minus_means(q):
             neg = stats.tile([P, QUAD], F32, name="neg_mean")
             nc.scalar.activation(
                 out=neg[:], in_=tiles["y_sum", q][:], func=ACT.Copy, scale=-1.0 / E
             )
-            scaled_columns("shift", q, neg[:], tiles["gain", q][:])
+            tiles["neg_mean", q] = neg
+
+        def gains_on_scalar(q):
+            scaled_columns("gain", q, mask[:, QUAD * q : QUAD * (q + 1)], tiles["rstd", q][:])
+
+        def shifts_on_scalar(q, count):
+            scaled_columns("shift", q, tiles["neg_mean", q][:], tiles["gain", q][:], count)
 
         def centre_times_g(k, r, g_psum):
             if r == 0:
@@ -508,9 +509,9 @@ def tile_edgefeaturenet_pb_t_kernel(
             nc.vector.scalar_tensor_tensor(
                 out=tiles["normed", k][:, r, :],
                 in0=y_pair(k)[:, r, :],
-                scalar=tiles["mean", k // 2][:, c : c + 1],
+                scalar=tiles["neg_mean", k // 2][:, c : c + 1],
                 in1=g_psum[:],
-                op0=ALU.subtract,
+                op0=ALU.add,
                 op1=ALU.mult,
             )
 
@@ -562,12 +563,17 @@ def tile_edgefeaturenet_pb_t_kernel(
             layer1(0, 1)
             layer1(0, 2, spare_bank=True)
             layer1(0, 3, spare_bank=True)
+            bank_b = psum_c.tile([P, E], F32, name="correction")
+            repeat_on_all_partitions(0, bank_b)
+            bank_g = psum_c.tile([P, E], F32, name="correction")
+            repeat_on_all_partitions(1, bank_g)
             transpose_h1(2)
             transpose_h1(3)
             bias_relu(0, 0)
             bias_relu(0, 1, on_vector=True)
             bias_relu(0, 2)
             bias_relu(0, 3, on_vector=True)
+            nc.scalar.copy(out=b3_row[:], in_=bank_b[:])
             group_h1(2)
             group_h1(3)
             group_h(0, 0)
@@ -575,29 +581,13 @@ def tile_edgefeaturenet_pb_t_kernel(
             transpose_h1(4)
             transpose_h1(5)
             quantise_h1(1)
-            bank = psum_c.tile([P, E], F32, name="correction")
-            repeat_on_all_partitions(0, bank)
             layer1(1, 0)
             layer1(1, 1)
             quantise_h(0, 0)
             quantise_h(0, 1)
-            nc.scalar.copy(out=b3_row[:], in_=bank[:])
             layer2(0)
-            group_h1(4)
-            group_h1(5)
-            bias_relu(1, 0)
-            bias_relu(1, 1, on_vector=True)
-            layer1(1, 2)
-            layer1(1, 3)
-            bank = psum_c.tile([P, E], F32, name="correction")
-            repeat_on_all_partitions(1, bank)
-            transpose_h1(6)
-            transpose_h1(7)
-            bias_relu(1, 2)
-            add_b3(0)
-            bias_relu(1, 3, on_vector=True)
             for r in range(PAIR):
-                nc.scalar.copy(out=g_rows[:, PAIR + r, :], in_=bank[:])
+                nc.scalar.copy(out=g_rows[:, PAIR + r, :], in_=bank_g[:])
             nc.gpsimd.tensor_scalar(
                 out=g_rows[:, 0:PAIR, :],
                 in0=g_rows[:, PAIR:QUAD, :],
@@ -606,6 +596,17 @@ def tile_edgefeaturenet_pb_t_kernel(
                 op0=ALU.mult,
                 op1=ALU.add,
             )
+            bias_relu(1, 0)
+            bias_relu(1, 1, on_vector=True)
+            layer1(1, 2)
+            layer1(1, 3)
+            group_h1(4)
+            group_h1(5)
+            transpose_h1(6)
+            transpose_h1(7)
+            bias_relu(1, 2)
+            add_b3(0)
+            bias_relu(1, 3)
             group_h(1, 2)
             mask = keep.tile([P, TILES], F32, name="mask")
             nc.vector.tensor_copy(out=mask[:], in_=mask_bf[:])
@@ -622,55 +623,70 @@ def tile_edgefeaturenet_pb_t_kernel(
                 pair(finish, k - 4)
                 if k % 2 == 0:
                     q = k // 2
+                    corrected = k - 2 < CORRECTED
                     pair(layer2, k + 1)
                     pair(group_h1, k + 6)
                     pair(group_h1, k + 7)
-                    pair(deviations, k, (0,))
+                    if k + 6 >= PAIRS:
+                        deviations(k)
                     quad(gains, q - 1)
                     quad(quantise_h1, q + 2)
-                    quad(shifts, q - 1)
+                    if k > CORRECTED:
+                        quad(shifts, q - 1)
                     quad(group_h, q + 1, 0)
                     quad(group_h, q + 1, 1)
                     quad(quantise_h, q + 1, 0)
-                    if k - 1 < CORRECTED:
-                        hold_group(q)
+                    if k > CORRECTED:
+                        hold_pair(max(k - 2, CORRECTED))
+                    elif k == 0:
+                        scale_group(q)
+                    else:
+                        shifts(q - 1)
                     quad(quantise_h, q + 1, 1)
                     quad(layer1, q + 2, 0)
                     quad(layer1, q + 2, 1)
+                    quad(bias_relu, q + 2, 0)
+                    quad(bias_relu, q + 2, 1, q + 2 == 2)
                     if 0 <= k - 2 < CORRECTED:
-                        first_piece(q - 1)
-                    pair(deviations, k, (1,))
-                    if 0 <= k - 2 < CORRECTED:
-                        first_rest(q - 1)
+                        if k > CORRECTED:
+                            nc.scalar.copy(out=columns[:, q - 1, 0:QUAD], in_=tiles["shift", q - 1][:])
+                        else:
+                            first_piece(q - 1)
+                    if 0 < k and k - 1 < CORRECTED:
+                        scale_group(q)
                     for i in (k - 2, k - 1):
                         if i >= CORRECTED:
                             for r in range(PAIR):
                                 normalise(i, r, False)
-                    if k - 1 < CORRECTED:
-                        scale_group(q)
-                    for i in (k - 2, k - 1):
-                        if i >= CORRECTED:
                             scale_by_g(i)
                     if 0 <= k - 3 < CORRECTED:
                         correction(k - 3, 0)
                         correction(k - 3, 1)
+                    quad(layer1, q + 2, 2)
+                    quad(layer1, q + 2, 3)
+                    if 0 <= k - 2 < CORRECTED:
+                        what_is_left(q - 1, 1)
                 else:
                     q = (k + 3) // 2
                     p = (k - 3) // 2
-                    quad(bias_relu, q, 0)
-                    quad(layer1, q, 2)
-                    if 0 <= 2 * p < CORRECTED:
-                        second_piece(p)
-                    quad(bias_relu, q, 1)
-                    pair(layer2, k + 1)
-                    quad(layer1, q, 3)
-                    if 0 <= 2 * p < CORRECTED:
-                        third_piece(p)
-                    pair(deviations, k)
-                    if 0 <= 2 * p < CORRECTED:
-                        coefficients(p)
-                    quad(reciprocal_std, (k - 1) // 2)
+                    corrected = 0 <= 2 * p < CORRECTED
+                    if k + 5 < PAIRS:
+                        deviations(k - 1)
+                    if corrected:
+                        next_piece(p, 1)
+                    pair(layer2, k + 1, (0,))
+                    if corrected:
+                        what_is_left(p, 2)
                     quad(bias_relu, q, 2)
+                    pair(layer2, k + 1, (1,))
+                    if corrected:
+                        next_piece(p, 2)
+                        turn(p)
+                    deviations(k, (0,))
+                    if corrected:
+                        coefficients(p)
+                    deviations(k, (1,))
+                    reciprocal_std(k // 2)
                     quad(bias_relu, q, 3)
                     quad(group_h, q, 2)
                     if 0 <= k - 3 < CORRECTED:
@@ -683,7 +699,9 @@ def tile_edgefeaturenet_pb_t_kernel(
             add_b3(last - 1)
             layer2(last)
             repeat_on_all_partitions(1, g_psum)
-            small_on_scalar(QUADS - 2)
+            minus_means(QUADS - 2)
+            gains_on_scalar(QUADS - 2)
+            shifts_on_scalar(QUADS - 2, QUAD)
             add_b3(last)
             normalise(last - 3, 0, False)
             normalise(last - 3, 1, False)
@@ -693,9 +711,10 @@ def tile_edgefeaturenet_pb_t_kernel(
             scale_by_g(last - 2)
             deviations(last - 1)
             deviations(last)
-            means(QUADS - 1)
+            minus_means(QUADS - 1)
             reciprocal_std(QUADS - 1)
-            small_on_scalar(QUADS - 1)
+            gains_on_scalar(QUADS - 1)
+            shifts_on_scalar(QUADS - 1, PAIR)
             add_beta_first(last - 5)
             add_beta_second_and_store(last - 5)
             add_beta_first(last - 4)

@@ -20,12 +20,10 @@ PAIRS = TILES // PAIR
 QUAD = 4
 QUADS = TILES // QUAD
 EPS = 1e-5
-CORRECTED = 23
-VECTOR_TOKENS = 352
+CORRECTED = 25
+VECTOR_TOKENS = 336
 EARLY_QUADS = 3
 HALF = 256
-LATE_QUADS = 13
-LATE_TOKENS = 448
 
 FLOPS = 2 * 2 * TOKENS * E * E
 
@@ -92,13 +90,14 @@ def tile_edgefeaturenet_pb_t_kernel(
         w2_words, w2_plane = load_weight(nc, keep, W2_words, W2_scales, "w2")
         b2_bf = keep.tile([P, PACK], BF16, name="b2_bf")
         nc.sync.dma_start(out=b2_bf[:], in_=b2.rearrange("(p t) -> p t", t=PACK))
-        load_h1(1)
-        vectors = keep.tile([P, 3, E], BF16, name="vectors")
-        nc.vector.memset(vectors[:].rearrange("p v n -> p (v n)").bitcast(I32), 0)
+        vector_rows = keep.tile([P, P], BF16, name="vector_rows")
+        nc.vector.memset(vector_rows[:].bitcast(I32), 0)
         for v, vector_dram in enumerate((b3, ln_g, ln_b)):
             nc.sync.dma_start(
-                out=vectors[0:1, v, :], in_=vector_dram.rearrange("(o n) -> o n", o=1)
+                out=vector_rows[4 * v : 4 * v + 4, :],
+                in_=vector_dram.rearrange("(c p) -> c p", p=P),
             )
+        load_h1(1)
         w3_words, w3_plane = load_weight(nc, keep, W3_words, W3_scales, "w3")
         load_h1(2)
         mask_bf = keep.tile([P, TILES], BF16, name="mask_bf")
@@ -111,9 +110,9 @@ def tile_edgefeaturenet_pb_t_kernel(
         ident_bf = keep.tile([P, P], BF16, name="ident_bf")
         make_identity(nc, ident_bf[:])
         minus_ident = keep.tile([P, P], BF16, name="minus_ident")
-        nc.scalar.mul(minus_ident[:], ident_bf[:], -1.0)
-        ones = keep.tile([P, P], BF16, name="ones")
-        nc.gpsimd.memset(ones[:], 1.0)
+        nc.gpsimd.tensor_scalar(
+            out=minus_ident[:], in0=ident_bf[:], scalar1=-1.0, scalar2=0.0, op0=ALU.mult, op1=ALU.add
+        )
 
         g_rows = keep.tile([P, QUAD, E], F32, name="g_rows")
         b3_row = keep.tile([P, E], BF16, name="b3_row")
@@ -131,8 +130,21 @@ def tile_edgefeaturenet_pb_t_kernel(
                 in_=ln_b.rearrange("(o n) -> o n", o=1),
             )
 
-        def repeat_on_all_partitions(v, bank):
-            nc.tensor.matmul(bank[:], lhsT=ones[:], rhs=vectors[:, v, :], start=True, stop=True)
+        vector_cols = keep.tile([P, 12], BF16, name="vector_cols")
+
+        def turn_vectors():
+            turned = psum_c.tile([P, P], BF16, name="correction")
+            nc.tensor.transpose(turned[:], vector_rows[:], ident_bf[:])
+            nc.scalar.copy(out=vector_cols[:], in_=turned[:, 0:12])
+
+        def repeat_on_all_partitions(v):
+            bank = psum_c.tile([P, E], BF16, name="correction")
+            for c in range(4):
+                col = vector_cols[:, 4 * v + c : 4 * v + c + 1]
+                nc.tensor.transpose(
+                    bank[:, c * P : (c + 1) * P], col.to_broadcast([P, P]), ident_bf[:]
+                )
+            return bank
 
         tiles = {}
 
@@ -207,7 +219,7 @@ def tile_edgefeaturenet_pb_t_kernel(
                 tiles["h_grouped", q] = front.tile(
                     [P, QUAD * P * PACK], BF16, name="h_grouped", align_bytes=64
                 )
-            split = QUAD * P if q < EARLY_QUADS else VECTOR_TOKENS if q < LATE_QUADS else LATE_TOKENS
+            split = VECTOR_TOKENS if q >= EARLY_QUADS else QUAD * P
             first, stop = ((0, HALF), (HALF, split), (split, QUAD * P))[part]
             if first == stop:
                 return
@@ -558,15 +570,14 @@ def tile_edgefeaturenet_pb_t_kernel(
             transpose_h1(1)
             group_h1(0)
             group_h1(1)
+            turn_vectors()
             quantise_h1(0)
             layer1(0, 0)
             layer1(0, 1)
             layer1(0, 2, spare_bank=True)
             layer1(0, 3, spare_bank=True)
-            bank_b = psum_c.tile([P, E], F32, name="correction")
-            repeat_on_all_partitions(0, bank_b)
-            bank_g = psum_c.tile([P, E], F32, name="correction")
-            repeat_on_all_partitions(1, bank_g)
+            bank_b = repeat_on_all_partitions(0)
+            bank_g = repeat_on_all_partitions(1)
             transpose_h1(2)
             transpose_h1(3)
             bias_relu(0, 0)
@@ -616,8 +627,7 @@ def tile_edgefeaturenet_pb_t_kernel(
             )
             for k in range(0, PAIRS - 2):
                 if k == CORRECTED + 4:
-                    tiles["beta"] = psum_c.tile([P, E], F32, name="correction")
-                    repeat_on_all_partitions(2, tiles["beta"])
+                    tiles["beta"] = repeat_on_all_partitions(2)
                 if k > 0:
                     add_b3(k)
                 pair(finish, k - 4)
@@ -646,7 +656,7 @@ def tile_edgefeaturenet_pb_t_kernel(
                     quad(layer1, q + 2, 0)
                     quad(layer1, q + 2, 1)
                     quad(bias_relu, q + 2, 0)
-                    quad(bias_relu, q + 2, 1, q + 2 == 2)
+                    quad(bias_relu, q + 2, 1)
                     if 0 <= k - 2 < CORRECTED:
                         if k > CORRECTED:
                             nc.scalar.copy(out=columns[:, q - 1, 0:QUAD], in_=tiles["shift", q - 1][:])
@@ -663,9 +673,9 @@ def tile_edgefeaturenet_pb_t_kernel(
                         correction(k - 3, 0)
                         correction(k - 3, 1)
                     quad(layer1, q + 2, 2)
-                    quad(layer1, q + 2, 3)
                     if 0 <= k - 2 < CORRECTED:
                         what_is_left(q - 1, 1)
+                    quad(layer1, q + 2, 3)
                 else:
                     q = (k + 3) // 2
                     p = (k - 3) // 2
@@ -695,10 +705,9 @@ def tile_edgefeaturenet_pb_t_kernel(
                     pair(transpose_h1, k + 7)
                     pair(transpose_h1, k + 8)
             last = PAIRS - 1
-            g_psum = psum_c.tile([P, E], F32, name="correction")
             add_b3(last - 1)
             layer2(last)
-            repeat_on_all_partitions(1, g_psum)
+            g_psum = repeat_on_all_partitions(1)
             minus_means(QUADS - 2)
             gains_on_scalar(QUADS - 2)
             shifts_on_scalar(QUADS - 2, QUAD)

@@ -21,7 +21,7 @@ QUAD = 4
 QUADS = TILES // QUAD
 EPS = 1e-5
 CORRECTED = 25
-VECTOR_TOKENS = 336
+VECTOR_TOKENS = 320
 EARLY_QUADS = 3
 HALF = 256
 
@@ -618,7 +618,6 @@ def tile_edgefeaturenet_pb_t_kernel(
             bias_relu(1, 2)
             add_b3(0)
             bias_relu(1, 3)
-            group_h(1, 2)
             mask = keep.tile([P, TILES], F32, name="mask")
             nc.vector.tensor_copy(out=mask[:], in_=mask_bf[:])
             nc.vector.tensor_copy(
@@ -636,9 +635,12 @@ def tile_edgefeaturenet_pb_t_kernel(
                     corrected = k - 2 < CORRECTED
                     pair(layer2, k + 1)
                     pair(group_h1, k + 6)
+                    if k + 6 >= PAIRS:
+                        deviations(k, (0,))
+                    quad(group_h, q + 1, 2)
                     pair(group_h1, k + 7)
                     if k + 6 >= PAIRS:
-                        deviations(k)
+                        deviations(k, (1,))
                     quad(gains, q - 1)
                     quad(quantise_h1, q + 2)
                     if k > CORRECTED:
@@ -696,13 +698,15 @@ def tile_edgefeaturenet_pb_t_kernel(
                     if corrected:
                         coefficients(p)
                     deviations(k, (1,))
-                    reciprocal_std(k // 2)
+                    if k < 4:
+                        reciprocal_std(k // 2)
                     quad(bias_relu, q, 3)
-                    quad(group_h, q, 2)
+                    if k >= 4:
+                        reciprocal_std(k // 2)
+                    pair(transpose_h1, k + 7)
                     if 0 <= k - 3 < CORRECTED:
                         correction(k - 3, 0)
                         correction(k - 3, 1)
-                    pair(transpose_h1, k + 7)
                     pair(transpose_h1, k + 8)
             last = PAIRS - 1
             add_b3(last - 1)
@@ -719,8 +723,8 @@ def tile_edgefeaturenet_pb_t_kernel(
             normalise(last - 2, 1, False)
             scale_by_g(last - 2)
             deviations(last - 1)
-            deviations(last)
             minus_means(QUADS - 1)
+            deviations(last)
             reciprocal_std(QUADS - 1)
             gains_on_scalar(QUADS - 1)
             shifts_on_scalar(QUADS - 1, PAIR)

import concourse.mybir as mybir
from concourse.masks import make_identity

F32 = mybir.dt.float32
BF16 = mybir.dt.bfloat16
I32 = mybir.dt.int32
U32 = mybir.dt.uint32
U8 = mybir.dt.uint8
FP8X4 = mybir.dt.float8_e4m3fn_x4
ALU = mybir.AluOpType
ACT = mybir.ActivationFunctionType

P = 128
PACK = 4
E = 512
TOKENS = 2 * 64 * 64
TILES = TOKENS // P
PAIR = 2
PAIRS = TILES // PAIR
QUAD = 4
QUADS = TILES // QUAD
EPS = 1e-5
CORRECTED = 25
VECTOR_TOKENS = 320
EARLY_QUADS = 3
HALF = 256

FLOPS = 2 * 2 * TOKENS * E * E


def load_weight(nc, keep, words_dram, scales_dram, name):
    words = keep.tile([P, PACK * E], U8, name=name + "_words", align_bytes=64)
    nc.sync.dma_start(
        out=words[:].bitcast(I32),
        in_=words_dram.rearrange("g p n t -> (g p) (n t)").bitcast(I32),
    )
    plane = keep.tile([P, E], U8, name=name + "_plane", align_bytes=64)
    nc.vector.memset(plane[:].bitcast(I32), 0)
    for quadrant in range(4):
        nc.sync.dma_start(
            out=plane[32 * quadrant : 32 * quadrant + 4, :].bitcast(I32),
            in_=scales_dram[0, 4 * quadrant : 4 * quadrant + 4, :].bitcast(I32),
        )
    return words, plane


def quantise_quad(nc, pool, grouped, name):
    codes = pool.tile([P, QUAD * P], U32, name=name + "_codes", align_bytes=64)
    scales = pool.tile([P, QUAD * P], U8, name=name + "_scales", align_bytes=64)
    nc.vector.quantize_mx(out=codes[:].bitcast(FP8X4), scales=scales[:], in_=grouped[:])
    return codes, scales


def tile_edgefeaturenet_pb_t_kernel(
    tc, h1, edge_mask, W2_words, W2_scales, b2, W3_words, W3_scales, b3, ln_g, ln_b, out
):
    nc = tc.nc
    h1_rows = h1.flatten_outer_dims().rearrange("(p i) k -> p i k", i=TILES)
    out_rows = out.flatten_outer_dims().rearrange("(p i) n -> p i n", i=TILES)
    mask_rows = edge_mask.rearrange("b r c -> (b r c)").rearrange("(p i) -> p i", i=TILES)

    with tc.tile_pool(name="keep", bufs=1) as keep, tc.tile_pool(
        name="front", bufs=3
    ) as front, tc.tile_pool(name="rows", bufs=4) as rows, tc.tile_pool(
        name="late", bufs=4
    ) as late, tc.tile_pool(
        name="groups", bufs=3
    ) as groups, tc.tile_pool(name="products", bufs=2) as products, tc.tile_pool(name="stats", bufs=3) as stats, tc.psum_pool(name="psum_t", bufs=2) as psum_t, tc.psum_pool(
        name="psum_x", bufs=2
    ) as psum_x, tc.psum_pool(name="psum_y", bufs=2) as psum_y, tc.psum_pool(
        name="psum_c", bufs=2
    ) as psum_c:
        eps = keep.tile([P, 1], F32, name="eps")
        nc.vector.memset(eps[:], EPS)
        warm = keep.tile([P, 1], F32, name="warm")
        nc.scalar.activation(out=warm[:], in_=eps[:], func=ACT.Abs_reciprocal_sqrt)

        h1_sb = []
        for q in range(QUADS):
            h1_sb.append(keep.tile([P, QUAD, E], BF16, name="h1_sb%d" % q))

        def load_h1(q, first=0, count=QUAD):
            i = q * QUAD + first
            nc.sync.dma_start(
                out=h1_sb[q][:, first : first + count, :], in_=h1_rows[:, i : i + count, :]
            )

        load_h1(0, 0, PAIR)
        load_h1(0, PAIR, PAIR)
        w2_words, w2_plane = load_weight(nc, keep, W2_words, W2_scales, "w2")
        b2_bf = keep.tile([P, PACK], BF16, name="b2_bf")
        nc.sync.dma_start(out=b2_bf[:], in_=b2.rearrange("(p t) -> p t", t=PACK))
        vector_rows = keep.tile([P, P], BF16, name="vector_rows")
        nc.vector.memset(vector_rows[:].bitcast(I32), 0)
        for v, vector_dram in enumerate((b3, ln_g, ln_b)):
            nc.sync.dma_start(
                out=vector_rows[4 * v : 4 * v + 4, :],
                in_=vector_dram.rearrange("(c p) -> c p", p=P),
            )
        load_h1(1)
        w3_words, w3_plane = load_weight(nc, keep, W3_words, W3_scales, "w3")
        load_h1(2)
        mask_bf = keep.tile([P, TILES], BF16, name="mask_bf")
        nc.sync.dma_start(out=mask_bf[:], in_=mask_rows)
        for q in range(3, QUADS):
            load_h1(q)

        ident_f32 = keep.tile([P, P], F32, name="ident_f32")
        make_identity(nc, ident_f32[:])
        ident_bf = keep.tile([P, P], BF16, name="ident_bf")
        make_identity(nc, ident_bf[:])
        minus_ident = keep.tile([P, P], BF16, name="minus_ident")
        nc.gpsimd.tensor_scalar(
            out=minus_ident[:], in0=ident_bf[:], scalar1=-1.0, scalar2=0.0, op0=ALU.mult, op1=ALU.add
        )

        g_rows = keep.tile([P, QUAD, E], F32, name="g_rows")
        b3_row = keep.tile([P, E], BF16, name="b3_row")

        columns = keep.tile([P, QUADS, P], BF16, name="columns")
        nc.vector.memset(columns[:].rearrange("p q c -> p (q c)").bitcast(I32), 0)
        gains_rows = keep.tile([P, QUAD, E], BF16, name="gains_rows")
        nc.vector.memset(gains_rows[:].rearrange("p c n -> p (c n)").bitcast(I32), 0)
        for c in range(QUAD):
            nc.sync.dma_start(
                out=gains_rows[c : 4 * QUAD : QUAD, c, :], in_=ln_g.partition_broadcast(4)
            )
            nc.sync.dma_start(
                out=gains_rows[4 * QUAD + c : 4 * QUAD + c + 1, c, :],
                in_=ln_b.rearrange("(o n) -> o n", o=1),
            )

        vector_cols = keep.tile([P, 12], BF16, name="vector_cols")

        def turn_vectors():
            turned = psum_c.tile([P, P], BF16, name="correction")
            nc.tensor.transpose(turned[:], vector_rows[:], ident_bf[:])
            nc.scalar.copy(out=vector_cols[:], in_=turned[:, 0:12])

        def repeat_on_all_partitions(v):
            bank = psum_c.tile([P, E], BF16, name="correction")
            for c in range(4):
                col = vector_cols[:, 4 * v + c : 4 * v + c + 1]
                nc.tensor.transpose(
                    bank[:, c * P : (c + 1) * P], col.to_broadcast([P, P]), ident_bf[:]
                )
            return bank

        tiles = {}

        def transpose_h1(k):
            h1T = psum_t.tile([P, PAIR, 2, P], F32, name="h1T")
            for r in range(PAIR):
                i = PAIR * k + r
                words = h1_sb[i // QUAD][:, i % QUAD, :].bitcast(F32)
                for u in range(2):
                    nc.tensor.transpose(h1T[:, r, u, :], words[:, u : E // 2 : 2], ident_f32[:])
            tiles["h1T", k] = h1T

        def group_h1(k, on_vector=False):
            q, half = k // 2, k % 2
            if half == 0:
                tiles["h1_grouped", q] = front.tile(
                    [P, QUAD * P * PACK], BF16, name="h1_grouped", align_bytes=64
                )
            words = tiles["h1_grouped", q][:].bitcast(F32)
            source = tiles["h1T", k][:].rearrange("p r u w -> p r w u")
            target = words[:, half * PAIR * P * 2 : (half + 1) * PAIR * P * 2].rearrange(
                "p (r w u) -> p r w u", r=PAIR, u=2
            )
            if on_vector:
                nc.vector.tensor_copy(out=target, in_=source)
            else:
                nc.scalar.copy(out=target, in_=source)

        def quantise_h1(q):
            tiles["h1_mx", q] = quantise_quad(nc, front, tiles["h1_grouped", q], "h1")

        def layer1(q, t, spare_bank=False):
            codes, scales = tiles["h1_mx", q]
            feature_cols = slice(t * P, (t + 1) * P)
            if spare_bank:
                product = psum_y.tile([P, QUAD * P], F32, name="x2")
            else:
                product = psum_x.tile([P, QUAD * P], F32, name="x1")
            nc.tensor.matmul_mx(
                out=product[:],
                lhsT=w2_sorted[:, feature_cols].bitcast(FP8X4),
                lhsT_scale=w2_sorted_plane[:, feature_cols],
                rhs=codes[:].bitcast(FP8X4),
                rhs_scale=scales[:],
                start=True,
                stop=True,
            )
            tiles["x1", q, t] = product

        def bias_relu(q, t, on_vector=False):
            if t == 0:
                tiles["h_by_t", q] = front.tile([P, PACK, QUAD * P], BF16, name="h_by_t")
            if on_vector:
                nc.vector.tensor_scalar(
                    out=tiles["h_by_t", q][:, t, :],
                    in0=tiles["x1", q, t][:],
                    scalar1=b2_cols[:, t : t + 1],
                    scalar2=0.0,
                    op0=ALU.add,
                    op1=ALU.max,
                )
            else:
                nc.scalar.activation(
                    out=tiles["h_by_t", q][:, t, :],
                    in_=tiles["x1", q, t][:],
                    func=ACT.Relu,
                    bias=b2_cols[:, t : t + 1],
                )

        def group_h(q, part):
            if ("h_grouped", q) not in tiles:
                tiles["h_grouped", q] = front.tile(
                    [P, QUAD * P * PACK], BF16, name="h_grouped", align_bytes=64
                )
            split = VECTOR_TOKENS if q >= EARLY_QUADS else QUAD * P
            first, stop = ((0, HALF), (HALF, split), (split, QUAD * P))[part]
            if first == stop:
                return
            target = tiles["h_grouped", q][:, PACK * first : PACK * stop].rearrange(
                "p (c i t) -> p c t i", i=4, t=PACK
            )
            source = tiles["h_by_t", q][:, :, first:stop].rearrange("p t (c i) -> p c t i", i=4)
            if part == 2:
                nc.scalar.copy(out=target, in_=source)
            else:
                nc.vector.tensor_copy(out=target, in_=source)

        def quantise_h(q, half):
            if half == 0:
                tiles["h_mx", q] = (
                    front.tile([P, QUAD * P], U32, name="h_codes", align_bytes=64),
                    front.tile([P, QUAD * P], U8, name="h_scales", align_bytes=64),
                )
            codes, scales = tiles["h_mx", q]
            cols = slice(half * HALF, (half + 1) * HALF)
            nc.vector.quantize_mx(
                out=codes[:, cols].bitcast(FP8X4),
                scales=scales[:, cols],
                in_=tiles["h_grouped", q][:, PACK * cols.start : PACK * cols.stop],
            )

        def layer2(k, tiles_of_pair=range(PAIR)):
            codes, scales = tiles["h_mx", k // 2]
            for r in tiles_of_pair:
                first = (PAIR * (k % 2) + r) * P
                token_cols = slice(first, first + P)
                product = psum_y.tile([P, E], F32, name="x2")
                nc.tensor.matmul_mx(
                    out=product[:],
                    lhsT=codes[:, token_cols].bitcast(FP8X4),
                    lhsT_scale=scales[:, token_cols],
                    rhs=w3_words[:].bitcast(FP8X4),
                    rhs_scale=w3_plane[:],
                    start=True,
                    stop=True,
                )
                tiles["x2", k, r] = product

        def span(k):
            first = PAIR * ((k + 1) % 2)
            return slice(first, first + PAIR)

        def y_pair(k):
            j = (k + 1) // 2
            if ("y", j) not in tiles:
                tiles["y", j] = groups.tile([P, QUAD, E], F32, name="y")
            return tiles["y", j][:, span(k), :]

        def hold_pair(k):
            tiles["scaled", k] = late.tile([P, PAIR, E], F32, name="scaled")[:]
            nc.vector.memset(tiles["scaled", k][:, 0, 0:1], 0.0)

        def scale_group(j):
            pairs = [k for k in (2 * j - 1, 2 * j) if 0 <= k < CORRECTED]
            first, last_slot = span(pairs[0]).start, span(pairs[-1]).stop
            scaled = products.tile([P, QUAD, E], F32, name="scaled_group")
            if j == 0:
                nc.vector.memset(scaled[:, span(0).start, 0:1], 0.0)
            nc.gpsimd.tensor_tensor(
                out=scaled[:, first:last_slot, :],
                in0=tiles["y", j][:, first:last_slot, :],
                in1=g_rows[:, first:last_slot, :],
                op=ALU.mult,
            )
            for k in pairs:
                tiles["scaled", k] = scaled[:, span(k), :]

        def scale_on_vector(k, g_psum):
            scaled = late.tile([P, PAIR, E], F32, name="scaled")
            for r in range(PAIR):
                nc.vector.tensor_tensor(
                    out=scaled[:, r, :], in0=y_pair(k)[:, r, :], in1=g_psum[:], op=ALU.mult
                )
            tiles["scaled", k] = scaled[:]

        def add_b3(k):
            q, half = k // 2, k % 2
            if half == 0:
                tiles["y_sum", q] = stats.tile([P, QUAD], F32, name="y_sum")
            y = y_pair(k)
            for r in range(PAIR):
                c = PAIR * half + r
                nc.vector.scalar_tensor_tensor(
                    out=y[:, r, :],
                    in0=tiles["x2", k, r][:],
                    scalar=1.0,
                    in1=b3_row[:],
                    op0=ALU.mult,
                    op1=ALU.add,
                    accum_out=tiles["y_sum", q][:, c : c + 1],
                )

        def deviations(k, tiles_of_pair=range(PAIR)):
            q, half = k // 2, k % 2
            if half == 0 and 0 in tiles_of_pair:
                tiles["dev_sq_sum", q] = stats.tile([P, QUAD], F32, name="dev_sq_sum")
            for r in tiles_of_pair:
                c = PAIR * half + r
                dev_sq = front.tile([P, E], BF16, name="dev_sq")
                nc.scalar.activation(
                    out=dev_sq[:],
                    in_=y_pair(k)[:, r, :],
                    func=ACT.Square,
                    scale=-1.0 * E,
                    bias=tiles["y_sum", q][:, c : c + 1],
                    accum_out=tiles["dev_sq_sum", q][:, c : c + 1],
                )

        def reciprocal_std(q):
            rstd = stats.tile([P, QUAD], F32, name="rstd")
            nc.scalar.activation(
                out=rstd[:],
                in_=tiles["dev_sq_sum", q][:],
                func=ACT.Abs_reciprocal_sqrt,
                scale=1.0 / (E * E * E),
                bias=eps[:],
            )
            tiles["rstd", q] = rstd

        def gains(q):
            gain = stats.tile([P, QUAD], F32, name="gain")
            nc.vector.tensor_tensor(
                out=gain[:],
                in0=tiles["rstd", q][:],
                in1=mask[:, QUAD * q : QUAD * (q + 1)],
                op=ALU.mult,
            )
            tiles["gain", q] = gain

        def shifts(q):
            shift = stats.tile([P, QUAD], F32, name="shift")
            nc.vector.scalar_tensor_tensor(
                out=shift[:],
                in0=tiles["y_sum", q][:],
                scalar=-1.0 / E,
                in1=tiles["gain", q][:],
                op0=ALU.mult,
                op1=ALU.mult,
            )
            tiles["shift", q] = shift

        def normalise(k, r, on_vector):
            if r == 0:
                tiles["normed", k] = late.tile([P, PAIR, E], F32, name="normed")
            c = PAIR * (k % 2) + r
            gain = tiles["gain", k // 2][:, c : c + 1]
            shift = tiles["shift", k // 2][:, c : c + 1]
            if on_vector:
                nc.vector.tensor_scalar(
                    out=tiles["normed", k][:, r, :],
                    in0=y_pair(k)[:, r, :],
                    scalar1=gain,
                    scalar2=shift,
                    op0=ALU.mult,
                    op1=ALU.add,
                )
            else:
                nc.scalar.activation(
                    out=tiles["normed", k][:, r, :],
                    in_=y_pair(k)[:, r, :],
                    func=ACT.Identity,
                    scale=gain,
                    bias=shift,
                )

        def scale_by_g(k):
            if ("scaled", k) not in tiles:
                tiles["scaled", k] = late.tile([P, PAIR, E], F32, name="scaled")[:]
            nc.gpsimd.tensor_tensor(
                out=tiles["scaled", k],
                in0=tiles["normed", k][:],
                in1=g_rows[:, 0:PAIR, :],
                op=ALU.mult,
            )

        def add_beta(k, r):
            if r == 0:
                tiles["result", k] = rows.tile([P, PAIR, E], F32, name="result")
            i = PAIR * k + r
            nc.vector.scalar_tensor_tensor(
                out=tiles["result", k][:, r, :],
                in0=tiles["beta"][:],
                scalar=mask[:, i : i + 1],
                in1=tiles["scaled", k][:, r, :],
                op0=ALU.mult,
                op1=ALU.add,
            )

        def add_beta_first(k):
            add_beta(k, 0)

        def add_beta_second_and_store(k):
            add_beta(k, 1)
            nc.sync.dma_start(
                out=out_rows[:, PAIR * k : PAIR * (k + 1), :], in_=tiles["result", k][:]
            )

        def first_piece(q):
            nc.gpsimd.tensor_copy(out=columns[:, q, 0:QUAD], in_=tiles["shift", q][:])

        def what_is_left(q, pieces):
            left = psum_t.tile([P, QUAD], F32, name="h1T")
            nc.tensor.matmul(
                left[:], lhsT=ident_f32[:], rhs=tiles["shift", q][:], start=True, stop=False
            )
            for j in range(pieces):
                nc.tensor.matmul(
                    left[:],
                    lhsT=minus_ident[:],
                    rhs=columns[:, q, j * QUAD : (j + 1) * QUAD],
                    start=False,
                    stop=j == pieces - 1,
                )
            tiles["left", q] = left

        def next_piece(q, j):
            nc.scalar.copy(
                out=columns[:, q, j * QUAD : (j + 1) * QUAD], in_=tiles["left", q][:]
            )

        def turn(q):
            turned = psum_t.tile([P, P], BF16, name="h1T")
            nc.tensor.transpose(turned[:], columns[:, q, :], ident_bf[:])
            tiles["turned", q] = turned

        def coefficients(q):
            rows_of_tokens = stats.tile([P, P], BF16, name="coefficients")
            nc.scalar.copy(out=rows_of_tokens[:], in_=tiles["turned", q][:])
            tiles["coefficients", q] = rows_of_tokens

        def correction(k, r):
            bank = psum_c.tile([P, E], F32, name="correction")
            nc.tensor.matmul(
                bank[:],
                lhsT=tiles["coefficients", k // 2][:],
                rhs=gains_rows[:, PAIR * (k % 2) + r, :],
                start=True,
                stop=True,
            )
            tiles["correction", k, r] = bank

        def add_correction(k, r):
            if r == 0:
                tiles["result", k] = rows.tile([P, PAIR, E], F32, name="result")
            c = PAIR * (k % 2) + r
            nc.vector.scalar_tensor_tensor(
                out=tiles["result", k][:, r, :],
                in0=tiles["scaled", k][:, r, :],
                scalar=tiles["gain", k // 2][:, c : c + 1],
                in1=tiles["correction", k, r][:],
                op0=ALU.mult,
                op1=ALU.add,
            )

        def finish(k):
            if k < CORRECTED:
                add_correction(k, 0)
                add_correction(k, 1)
            else:
                add_beta(k, 0)
                add_beta(k, 1)
            nc.sync.dma_start(
                out=out_rows[:, PAIR * k : PAIR * (k + 1), :], in_=tiles["result", k][:]
            )

        def scaled_columns(name, q, factors, source, count=QUAD):
            out_tile = stats.tile([P, QUAD], F32, name=name)
            for c in range(count):
                nc.scalar.activation(
                    out=out_tile[:, c : c + 1],
                    in_=source[:, c : c + 1],
                    func=ACT.Copy,
                    scale=factors[:, c : c + 1],
                )
            tiles[name, q] = out_tile

        def minus_means(q):
            neg = stats.tile([P, QUAD], F32, name="neg_mean")
            nc.scalar.activation(
                out=neg[:], in_=tiles["y_sum", q][:], func=ACT.Copy, scale=-1.0 / E
            )
            tiles["neg_mean", q] = neg

        def gains_on_scalar(q):
            scaled_columns("gain", q, mask[:, QUAD * q : QUAD * (q + 1)], tiles["rstd", q][:])

        def shifts_on_scalar(q, count):
            scaled_columns("shift", q, tiles["neg_mean", q][:], tiles["gain", q][:], count)

        def centre_times_g(k, r, g_psum):
            if r == 0:
                tiles["normed", k] = late.tile([P, PAIR, E], F32, name="normed")
            c = PAIR * (k % 2) + r
            nc.vector.scalar_tensor_tensor(
                out=tiles["normed", k][:, r, :],
                in0=y_pair(k)[:, r, :],
                scalar=tiles["neg_mean", k // 2][:, c : c + 1],
                in1=g_psum[:],
                op0=ALU.add,
                op1=ALU.mult,
            )

        def times_gain(k, r):
            if r == 0:
                tiles["scaled", k] = late.tile([P, PAIR, E], F32, name="scaled")[:]
            c = PAIR * (k % 2) + r
            nc.scalar.activation(
                out=tiles["scaled", k][:, r, :],
                in_=tiles["normed", k][:, r, :],
                func=ACT.Copy,
                scale=tiles["gain", k // 2][:, c : c + 1],
            )

        def add_beta_and_store_each(k):
            for r in range(PAIR):
                add_beta(k, r)
                nc.sync.dma_start(
                    out=out_rows[:, PAIR * k + r, :], in_=tiles["result", k][:, r, :]
                )

        def pair(stage, k, *more):
            if 0 <= k < PAIRS:
                stage(k, *more)

        def quad(stage, q, *more):
            if 0 <= q < QUADS:
                stage(q, *more)

        with tc.manual_schedule():
            w2_sorted = keep.tile([P, E], U32, name="w2_sorted", align_bytes=64)
            nc.vector.tensor_copy(
                out=w2_sorted[:].bitcast(I32).rearrange("p (t m) -> p t m", t=PACK),
                in_=w2_words[:].bitcast(I32).rearrange("p (m t) -> p t m", t=PACK),
            )
            w2_sorted_plane = keep.tile([P, E], U8, name="w2_sorted_plane", align_bytes=64)
            nc.vector.tensor_copy(
                out=w2_sorted_plane[:].rearrange("p (t m) -> p m t", t=PACK),
                in_=w2_plane[:].rearrange("p (m t) -> p m t", t=PACK),
            )
            b2_cols = keep.tile([P, PACK], F32, name="b2_cols")
            nc.vector.tensor_copy(out=b2_cols[:], in_=b2_bf[:])
            transpose_h1(0)
            transpose_h1(1)
            group_h1(0)
            group_h1(1)
            turn_vectors()
            quantise_h1(0)
            layer1(0, 0)
            layer1(0, 1)
            layer1(0, 2, spare_bank=True)
            layer1(0, 3, spare_bank=True)
            bank_b = repeat_on_all_partitions(0)
            bank_g = repeat_on_all_partitions(1)
            transpose_h1(2)
            transpose_h1(3)
            bias_relu(0, 0)
            bias_relu(0, 1, on_vector=True)
            bias_relu(0, 2)
            bias_relu(0, 3, on_vector=True)
            nc.scalar.copy(out=b3_row[:], in_=bank_b[:])
            group_h1(2)
            group_h1(3)
            group_h(0, 0)
            group_h(0, 1)
            transpose_h1(4)
            transpose_h1(5)
            quantise_h1(1)
            layer1(1, 0)
            layer1(1, 1)
            quantise_h(0, 0)
            quantise_h(0, 1)
            layer2(0)
            for r in range(PAIR):
                nc.scalar.copy(out=g_rows[:, PAIR + r, :], in_=bank_g[:])
            nc.gpsimd.tensor_scalar(
                out=g_rows[:, 0:PAIR, :],
                in0=g_rows[:, PAIR:QUAD, :],
                scalar1=1.0,
                scalar2=0.0,
                op0=ALU.mult,
                op1=ALU.add,
            )
            bias_relu(1, 0)
            bias_relu(1, 1, on_vector=True)
            layer1(1, 2)
            layer1(1, 3)
            group_h1(4)
            group_h1(5)
            transpose_h1(6)
            transpose_h1(7)
            bias_relu(1, 2)
            add_b3(0)
            bias_relu(1, 3)
            mask = keep.tile([P, TILES], F32, name="mask")
            nc.vector.tensor_copy(out=mask[:], in_=mask_bf[:])
            nc.vector.tensor_copy(
                out=columns[:, :, 4 * QUAD : 5 * QUAD],
                in_=mask_bf[:].rearrange("p (q c) -> p q c", c=QUAD),
            )
            for k in range(0, PAIRS - 2):
                if k == CORRECTED + 4:
                    tiles["beta"] = repeat_on_all_partitions(2)
                if k > 0:
                    add_b3(k)
                pair(finish, k - 4)
                if k % 2 == 0:
                    q = k // 2
                    corrected = k - 2 < CORRECTED
                    pair(layer2, k + 1)
                    pair(group_h1, k + 6)
                    if k + 6 >= PAIRS:
                        deviations(k, (0,))
                    quad(group_h, q + 1, 2)
                    pair(group_h1, k + 7)
                    if k + 6 >= PAIRS:
                        deviations(k, (1,))
                    quad(gains, q - 1)
                    quad(quantise_h1, q + 2)
                    if k > CORRECTED:
                        quad(shifts, q - 1)
                    quad(group_h, q + 1, 0)
                    quad(group_h, q + 1, 1)
                    quad(quantise_h, q + 1, 0)
                    if k > CORRECTED:
                        hold_pair(max(k - 2, CORRECTED))
                    elif k == 0:
                        scale_group(q)
                    else:
                        shifts(q - 1)
                    quad(quantise_h, q + 1, 1)
                    quad(layer1, q + 2, 0)
                    quad(layer1, q + 2, 1)
                    quad(bias_relu, q + 2, 0)
                    quad(bias_relu, q + 2, 1)
                    if 0 <= k - 2 < CORRECTED:
                        if k > CORRECTED:
                            nc.scalar.copy(out=columns[:, q - 1, 0:QUAD], in_=tiles["shift", q - 1][:])
                        else:
                            first_piece(q - 1)
                    if 0 < k and k - 1 < CORRECTED:
                        scale_group(q)
                    for i in (k - 2, k - 1):
                        if i >= CORRECTED:
                            for r in range(PAIR):
                                normalise(i, r, False)
                            scale_by_g(i)
                    if 0 <= k - 3 < CORRECTED:
                        correction(k - 3, 0)
                        correction(k - 3, 1)
                    quad(layer1, q + 2, 2)
                    if 0 <= k - 2 < CORRECTED:
                        what_is_left(q - 1, 1)
                    quad(layer1, q + 2, 3)
                else:
                    q = (k + 3) // 2
                    p = (k - 3) // 2
                    corrected = 0 <= 2 * p < CORRECTED
                    if k + 5 < PAIRS:
                        deviations(k - 1)
                    if corrected:
                        next_piece(p, 1)
                    pair(layer2, k + 1, (0,))
                    if corrected:
                        what_is_left(p, 2)
                    quad(bias_relu, q, 2)
                    pair(layer2, k + 1, (1,))
                    if corrected:
                        next_piece(p, 2)
                        turn(p)
                    deviations(k, (0,))
                    if corrected:
                        coefficients(p)
                    deviations(k, (1,))
                    if k < 4:
                        reciprocal_std(k // 2)
                    quad(bias_relu, q, 3)
                    if k >= 4:
                        reciprocal_std(k // 2)
                    pair(transpose_h1, k + 7)
                    if 0 <= k - 3 < CORRECTED:
                        correction(k - 3, 0)
                        correction(k - 3, 1)
                    pair(transpose_h1, k + 8)
            last = PAIRS - 1
            add_b3(last - 1)
            layer2(last)
            g_psum = repeat_on_all_partitions(1)
            minus_means(QUADS - 2)
            gains_on_scalar(QUADS - 2)
            shifts_on_scalar(QUADS - 2, QUAD)
            add_b3(last)
            normalise(last - 3, 0, False)
            normalise(last - 3, 1, False)
            scale_by_g(last - 3)
            normalise(last - 2, 0, False)
            normalise(last - 2, 1, False)
            scale_by_g(last - 2)
            deviations(last - 1)
            minus_means(QUADS - 1)
            deviations(last)
            reciprocal_std(QUADS - 1)
            gains_on_scalar(QUADS - 1)
            shifts_on_scalar(QUADS - 1, PAIR)
            add_beta_first(last - 5)
            add_beta_second_and_store(last - 5)
            add_beta_first(last - 4)
            add_beta_second_and_store(last - 4)
            add_beta_first(last - 3)
            add_beta_second_and_store(last - 3)
            centre_times_g(last, 0, g_psum)
            centre_times_g(last, 1, g_psum)
            normalise(last - 1, 0, False)
            normalise(last - 1, 1, False)
            scale_by_g(last - 1)
            times_gain(last, 0)
            times_gain(last, 1)
            add_beta_first(last - 2)
            add_beta_second_and_store(last - 2)
            add_beta_first(last)
            add_beta_second_and_store(last)
            add_beta_and_store_each(last - 1)
